import numpy as np
import ml_dtypes


def mxq(x, axis, fmt="e4m3"):
    dtype, down = {"e4m3": (ml_dtypes.float8_e4m3fn, 7), "e5m2": (ml_dtypes.float8_e5m2, 14)}[fmt]
    v = np.moveaxis(np.asarray(x, np.float32).astype(ml_dtypes.bfloat16).astype(np.float64), axis, -1)
    blocks = v.reshape(v.shape[:-1] + (-1, 32))
    amax = np.abs(blocks).max(-1, keepdims=True)
    byte = np.maximum(np.where(amax > 0, np.frexp(amax)[1] - 1 + 127, 0) - down, 1)
    scale = np.exp2(byte - 127.0)
    codes = (blocks / scale).astype(np.float32).astype(dtype).astype(np.float64)
    return np.moveaxis((codes * scale).reshape(v.shape), -1, axis)


WIDE = False


def mx_kscale(k):
    if not WIDE:
        return np.ones(k)
    levels = np.array([10, -10, 5, -5, 0])
    a = np.random.permutation(np.resize(levels, k // 512 * 4)).reshape(k // 512, 4)
    idx = np.arange(k)
    return np.exp2(a[idx // 512, idx % 128 // 32])


BF16 = ml_dtypes.bfloat16


def bf(x):
    return np.asarray(x, np.float32).astype(BF16)


def f64(x):
    return np.asarray(x).astype(np.float64)


B, N0, N1, N2, M0, M1, M2, QA, QB = 2, 16, 16, 16, 16, 16, 128, 8, 8
RA, RB = QA * QA, QB * QB
M = M0 * M1 * M2
T0 = B * M0
KA, KB = RA * M1, RB * M2
L = 1.0


def setup_inputs():
    s = mx_kscale(KA).reshape(RA, M1)
    d1 = np.random.standard_normal((RA, M1, M2, T0)) * 1.2 * s[:, :, None, None]
    g1 = np.random.standard_normal((RA, M1, M1, RB)) / np.sqrt(KA) / s[:, None, :, None]
    g2 = np.random.standard_normal((RB, M2, M2))[..., None] * 0.2 / np.sqrt(KB)
    return {'d1': bf(d1.reshape(RA, M1 * M2, T0)), 'g1': bf(g1), 'g2': bf(g2),
            'x_l': bf(np.random.standard_normal((B, M)) * 1.2), 'mv': bf(np.random.standard_normal((B, M))),
            'bias': bf(np.random.standard_normal(M) * 0.2)}


def reference(d1, g1, g2, x_l, mv, bias):
    a = f64(d1).reshape(KA, M2 * T0)
    w1 = f64(g1).transpose(0, 2, 3, 1).reshape(KA, RB * M1)
    y = mxq(a, 0, 'e4m3').T @ mxq(w1, 0, 'e4m3')
    d2 = y.reshape(M2, T0, RB, M1).transpose(2, 0, 1, 3).reshape(KB, T0 * M1)
    w2 = f64(g2).reshape(RB, M2, M2).transpose(0, 2, 1).reshape(KB, M2)
    term = (mxq(d2, 0, 'e4m3').T @ mxq(w2, 0, 'e4m3')).reshape(B, M)
    return f64(x_l) - term / L + f64(mv) / L + f64(bias)

@@ -1,0 +1,202 @@
+from contextlib import ExitStack
+
+import concourse.mybir as mybir
+from concourse.masks import make_identity
+
+FLOPS = 2 * 1024 * 4096 * 1024 + 2 * 8192 * 512 * 128
+
+BF16 = mybir.dt.bfloat16
+F32 = mybir.dt.float32
+U32 = mybir.dt.uint32
+U8 = mybir.dt.uint8
+FP8X4 = mybir.dt.float8_e4m3fn_x4
+ADD = mybir.AluOpType.add
+SUB = mybir.AluOpType.subtract
+P = 128
+
+V_TQ = 5
+
+
+def tile_ttsolver_pa_kernel(tc, d1, g1, g2, x_l, mv, bias, out):
+    nc = tc.nc
+    with ExitStack() as ctx:
+        raw16 = ctx.enter_context(tc.tile_pool(name="raw16", bufs=3))
+        big16 = ctx.enter_context(tc.tile_pool(name="big16", bufs=5))
+        s8 = ctx.enter_context(tc.tile_pool(name="s8", bufs=2))
+        keep = ctx.enter_context(tc.tile_pool(name="keep", bufs=1))
+        d2q = ctx.enter_context(tc.tile_pool(name="d2q", bufs=2))
+        ps1 = ctx.enter_context(tc.psum_pool(name="ps1", bufs=5))
+        pst = ctx.enter_context(tc.psum_pool(name="pst", bufs=2))
+        ps2 = ctx.enter_context(tc.psum_pool(name="ps2", bufs=1))
+
+        d1c = keep.tile([P, 8, 2, 512], U32, align_bytes=64)
+        d1s = keep.tile([P, 8, 2, 512], U8, align_bytes=64)
+        g1c = keep.tile([P, 2, 2, 512], U32, align_bytes=64)
+        g1s = keep.tile([P, 2, 2, 512], U8, align_bytes=64)
+        g2c = keep.tile([P, 16, 128], U32, align_bytes=64)
+        g2s = keep.tile([P, 16, 128], U8, align_bytes=64)
+        ident = keep.tile([P, P], BF16)
+        xt = keep.tile([P, 4, 128], BF16)
+        mt = keep.tile([P, 4, 128], BF16)
+        bt = keep.tile([P, 2, 128], BF16)
+        base = keep.tile([P, 4, 128], F32)
+
+        make_identity(nc, ident[:])
+
+        d1v = d1.rearrange("r (n a) t -> (r n) (a t)", n=16)
+        outv = out.rearrange("b (r j) -> (b r) j", j=128)
+
+        def load_g1(mh):
+            t_ = s8.tile([P, 2, 8, 256], BF16, tag="s8", name="g1raw%d" % mh, align_bytes=64)
+            for c in range(2):
+                for nh in range(4):
+                    nc.sync.dma_start(
+                        out=t_[nh:P:4, c, :, :],
+                        in_=g1[32 * c : 32 * c + 32, 8 * mh : 8 * mh + 8, 4 * nh : 4 * nh + 4, :].rearrange(
+                            "r m n s -> r m (n s)"
+                        ),
+                    )
+            return t_
+
+        def prep_g1(mh, raw):
+            grp = s8.tile([P, 2, 16, 8, 4, 4], BF16, tag="s8", name="g1grp%d" % mh, align_bytes=64)
+            for c in range(2):
+                nc.vector.tensor_copy(
+                    out=grp[:, c].rearrange("p sg m j n -> p m sg n j"),
+                    in_=raw[:, c].rearrange("p m (n sg j) -> p m sg n j", n=4, j=4),
+                )
+            nc.vector.quantize_mx(
+                out=g1c[:, mh].rearrange("p c w -> p (c w)").bitcast(FP8X4),
+                scales=g1s[:, mh].rearrange("p c w -> p (c w)"),
+                in_=grp[:].rearrange("p c sg m j n -> p (c sg m j n)"),
+            )
+
+        def load_d1(c, ah):
+            t_ = raw16.tile([P, 4, 2048], BF16, tag="raw16", name="d1raw%d%d" % (c, ah))
+            nc.sync.dma_start(
+                out=t_[:],
+                in_=d1v[512 * c : 512 * c + 512, 2048 * ah : 2048 * ah + 2048].rearrange("(p j) w -> p j w", j=4),
+            )
+            return t_
+
+        grouped = [
+            big16.tile([P, 2, 2, 4, 128, 4], BF16, tag="big16", name="d1grp%d" % q, align_bytes=64) for q in range(4)
+        ]
+
+        def units(c, ah, raw):
+            src = raw[:].rearrange("p j (a t) -> p a j t", t=32)
+            for tq in range(8):
+                dst = grouped[tq // 2][:, tq % 2, c, :, 64 * ah : 64 * ah + 64, :].rearrange("p t a j -> p a j t")
+                if tq < V_TQ:
+                    nc.vector.tensor_copy(out=dst, in_=src[:, :, :, 4 * tq : 4 * tq + 4])
+                else:
+                    nc.scalar.copy(out=dst, in_=src[:, :, :, 4 * tq : 4 * tq + 4])
+
+        def quant_d1(tq, c):
+            nc.vector.quantize_mx(
+                out=d1c[:, tq, c, :].bitcast(FP8X4),
+                scales=d1s[:, tq, c, :],
+                in_=grouped[tq // 2][:, tq % 2, c].rearrange("p t a j -> p (t a j)"),
+            )
+
+        g1raw0 = load_g1(0)
+        r00 = load_d1(0, 0)
+        r01 = load_d1(0, 1)
+        r10 = load_d1(1, 0)
+        prep_g1(0, g1raw0)
+        units(0, 0, r00)
+        r11 = load_d1(1, 1)
+        units(0, 1, r01)
+        g1raw1 = load_g1(1)
+        g2raw = raw16.tile([P, 64, 128], BF16, tag="raw16", name="g2raw")
+        nc.sync.dma_start(out=g2raw[:], in_=g2.rearrange("s (h l) a o -> (s h) l (a o)", h=2))
+        nc.sync.dma_start(out=xt[:], in_=x_l.rearrange("b (r j) -> (b r) j", j=128).rearrange("(q p) j -> p q j", p=P))
+        nc.sync.dma_start(out=mt[:], in_=mv.rearrange("b (r j) -> (b r) j", j=128).rearrange("(q p) j -> p q j", p=P))
+        nc.sync.dma_start(out=bt[:], in_=bias.rearrange("(h p j) -> p h j", p=P, j=128))
+        for tq in range(8):
+            quant_d1(tq, 0)
+        units(1, 0, r10)
+        units(1, 1, r11)
+
+        d2in = {}
+
+        def first_core(mh, t):
+            q, tl = t // 8, t % 8
+            acc = ps1.tile([P, 512], F32, tag="ps1", name="acc")
+            for c in range(2):
+                nc.tensor.matmul_mx(
+                    out=acc[:],
+                    lhsT=d1c[:, t // 4, c, 128 * (t % 4) : 128 * (t % 4) + 128].bitcast(FP8X4),
+                    lhsT_scale=d1s[:, t // 4, c, 128 * (t % 4) : 128 * (t % 4) + 128],
+                    rhs=g1c[:, mh, c, :].bitcast(FP8X4),
+                    rhs_scale=g1s[:, mh, c, :],
+                    start=(c == 0),
+                    stop=(c == 1),
+                )
+            dst = d2in[q][:, :, tl, 8 * mh : 8 * mh + 8, :]
+            src = acc[:].rearrange("p (sg m j) -> p sg m j", m=8, j=4)
+            if t % 4 == 3:
+                nc.vector.tensor_copy(out=dst, in_=src)
+            else:
+                nc.scalar.copy(out=dst, in_=src)
+
+        for t in range(32):
+            if t % 4 == 0:
+                quant_d1(t // 4, 1)
+            if t % 8 == 0:
+                d2in[t // 8] = big16.tile(
+                    [P, 16, 8, 16, 4], BF16, tag="big16", name="d2in%d" % (t // 8), align_bytes=64
+                )
+            first_core(0, t)
+
+        prep_g1(1, g1raw1)
+        nc.vector.tensor_tensor(out=base[:], in0=xt[:], in1=mt[:], op=ADD)
+        for b in range(2):
+            nc.vector.tensor_tensor(out=base[:, 2 * b : 2 * b + 2, :], in0=base[:, 2 * b : 2 * b + 2, :], in1=bt[:], op=ADD)
+
+        g2in = big16.tile([P, 16, 2, 64, 4], BF16, tag="big16", name="g2in", align_bytes=64)
+        for grp8 in range(8):
+            tp = pst.tile([P, 8, 128], BF16, tag="pst", name="tp")
+            for g in range(8):
+                nc.tensor.transpose(tp[:, g, :], g2raw[:, 8 * grp8 + g, :], ident[:])
+            for jh in range(2):
+                nc.scalar.copy(
+                    out=g2in[:, :, jh, 8 * grp8 : 8 * grp8 + 8, :],
+                    in_=tp[:].rearrange("p g (sg j h) -> p h sg g j", j=4, h=2)[:, jh],
+                )
+        for h in range(2):
+            nc.vector.quantize_mx(
+                out=g2c[:, 8 * h : 8 * h + 8, :].rearrange("p sg w -> p (sg w)").bitcast(FP8X4),
+                scales=g2s[:, 8 * h : 8 * h + 8, :].rearrange("p sg w -> p (sg w)"),
+                in_=g2in[:, 8 * h : 8 * h + 8].rearrange("p sg h l j -> p (sg h l j)"),
+            )
+
+        def second_core(q):
+            cod = d2q.tile([P, 16, 128], U32, tag="d2c", name="d2c", align_bytes=64)
+            sca = d2q.tile([P, 16, 128], U8, tag="d2s", name="d2s", align_bytes=64)
+            for h in range(2):
+                nc.vector.quantize_mx(
+                    out=cod[:, 8 * h : 8 * h + 8, :].rearrange("p sg w -> p (sg w)").bitcast(FP8X4),
+                    scales=sca[:, 8 * h : 8 * h + 8, :].rearrange("p sg w -> p (sg w)"),
+                    in_=d2in[q][:, 8 * h : 8 * h + 8].rearrange("p sg t m j -> p (sg t m j)"),
+                )
+            term = ps2.tile([P, 128], F32, tag="ps2", name="term")
+            for sg in range(16):
+                nc.tensor.matmul_mx(
+                    out=term[:],
+                    lhsT=cod[:, sg, :].bitcast(FP8X4),
+                    lhsT_scale=sca[:, sg, :],
+                    rhs=g2c[:, sg, :].bitcast(FP8X4),
+                    rhs_scale=g2s[:, sg, :],
+                    start=(sg == 0),
+                    stop=(sg == 15),
+                )
+            res = d2q.tile([P, 128], F32, tag="res", name="res")
+            nc.vector.tensor_tensor(out=res[:], in0=base[:, q, :], in1=term[:], op=SUB)
+            nc.sync.dma_start(out=outv[128 * q : 128 * q + 128, :], in_=res[:])
+
+        for t in range(32):
+            first_core(1, t)
+            if t % 8 == 3 and t >= 11:
+                second_core(t // 8 - 1)
+        second_core(3)

@@ -14,8 +14,6 @@ ADD = mybir.AluOpType.add
 SUB = mybir.AluOpType.subtract
 P = 128
 
-V_TQ = 5
-
 
 def tile_ttsolver_pa_kernel(tc, d1, g1, g2, x_l, mv, bias, out):
     nc = tc.nc
@@ -25,9 +23,8 @@ def tile_ttsolver_pa_kernel(tc, d1, g1, g2, x_l, mv, bias, out):
         s8 = ctx.enter_context(tc.tile_pool(name="s8", bufs=2))
         keep = ctx.enter_context(tc.tile_pool(name="keep", bufs=1))
         d2q = ctx.enter_context(tc.tile_pool(name="d2q", bufs=2))
-        ps1 = ctx.enter_context(tc.psum_pool(name="ps1", bufs=5))
-        pst = ctx.enter_context(tc.psum_pool(name="pst", bufs=2))
-        ps2 = ctx.enter_context(tc.psum_pool(name="ps2", bufs=1))
+        psum = ctx.enter_context(tc.psum_pool(name="psum", bufs=8))
+        ctx.enter_context(tc.manual_schedule())
 
         d1c = keep.tile([P, 8, 2, 512], U32, align_bytes=64)
         d1s = keep.tile([P, 8, 2, 512], U8, align_bytes=64)
@@ -58,39 +55,46 @@ def tile_ttsolver_pa_kernel(tc, d1, g1, g2, x_l, mv, bias, out):
                     )
             return t_
 
-        def prep_g1(mh, raw):
-            grp = s8.tile([P, 2, 16, 8, 4, 4], BF16, tag="s8", name="g1grp%d" % mh, align_bytes=64)
-            for c in range(2):
-                nc.vector.tensor_copy(
-                    out=grp[:, c].rearrange("p sg m j n -> p m sg n j"),
-                    in_=raw[:, c].rearrange("p m (n sg j) -> p m sg n j", n=4, j=4),
-                )
+        def g1_copy(grp, raw, c):
+            nc.vector.tensor_copy(
+                out=grp[:, c].rearrange("p sg m j n -> p m sg n j"),
+                in_=raw[:, c].rearrange("p m (n sg j) -> p m sg n j", n=4, j=4),
+            )
+
+        def g1_quant(grp, mh):
             nc.vector.quantize_mx(
                 out=g1c[:, mh].rearrange("p c w -> p (c w)").bitcast(FP8X4),
                 scales=g1s[:, mh].rearrange("p c w -> p (c w)"),
                 in_=grp[:].rearrange("p c sg m j n -> p (c sg m j n)"),
             )
 
-        def load_d1(c, ah):
+        def load_d1(c, ah, pieces):
             t_ = raw16.tile([P, 4, 2048], BF16, tag="raw16", name="d1raw%d%d" % (c, ah))
-            nc.sync.dma_start(
-                out=t_[:],
-                in_=d1v[512 * c : 512 * c + 512, 2048 * ah : 2048 * ah + 2048].rearrange("(p j) w -> p j w", j=4),
-            )
+            w = 2048 // pieces
+            for i in range(pieces):
+                nc.sync.dma_start(
+                    out=t_[:, :, w * i : w * i + w],
+                    in_=d1v[512 * c : 512 * c + 512, 2048 * ah + w * i : 2048 * ah + w * i + w].rearrange(
+                        "(p j) w -> p j w", j=4
+                    ),
+                )
             return t_
 
         grouped = [
             big16.tile([P, 2, 2, 4, 128, 4], BF16, tag="big16", name="d1grp%d" % q, align_bytes=64) for q in range(4)
         ]
 
-        def units(c, ah, raw):
-            src = raw[:].rearrange("p j (a t) -> p a j t", t=32)
-            for tq in range(8):
-                dst = grouped[tq // 2][:, tq % 2, c, :, 64 * ah : 64 * ah + 64, :].rearrange("p t a j -> p a j t")
-                if tq < V_TQ:
-                    nc.vector.tensor_copy(out=dst, in_=src[:, :, :, 4 * tq : 4 * tq + 4])
-                else:
-                    nc.scalar.copy(out=dst, in_=src[:, :, :, 4 * tq : 4 * tq + 4])
+        def unit(eng_copy, raw, c, a_dst, a_src, a_len, tq):
+            eng_copy(
+                out=grouped[tq // 2][:, tq % 2, c, :, a_dst : a_dst + a_len, :].rearrange("p t a j -> p a j t"),
+                in_=raw[:].rearrange("p j (a t) -> p a j t", t=32)[:, a_src : a_src + a_len, :, 4 * tq : 4 * tq + 4],
+            )
+
+        def units(raw, c, a_dst, a_src, a_len, n_vector):
+            for tq in range(n_vector):
+                unit(nc.vector.tensor_copy, raw, c, a_dst, a_src, a_len, tq)
+            for tq in range(n_vector, 8):
+                unit(nc.scalar.copy, raw, c, a_dst, a_src, a_len, tq)
 
         def quant_d1(tq, c):
             nc.vector.quantize_mx(
@@ -99,104 +103,179 @@ def tile_ttsolver_pa_kernel(tc, d1, g1, g2, x_l, mv, bias, out):
                 in_=grouped[tq // 2][:, tq % 2, c].rearrange("p t a j -> p (t a j)"),
             )
 
+        acc = {}
+        d2in = {}
+
+        def pass1(mh, t, c, lo=0, n=512):
+            nc.tensor.matmul_mx(
+                out=acc[t][:],
+                lhsT=d1c[:, t // 4, c, 128 * (t % 4) : 128 * (t % 4) + 128].bitcast(FP8X4),
+                lhsT_scale=d1s[:, t // 4, c, 128 * (t % 4) : 128 * (t % 4) + 128],
+                rhs=g1c[:, mh, c, lo : lo + n].bitcast(FP8X4),
+                rhs_scale=g1s[:, mh, c, lo : lo + n],
+                start=(c == 0),
+                stop=(c == 1),
+            )
+
+        def new_acc(t, n=512):
+            acc[t] = psum.tile([P, n], F32, tag="bank", name="acc")
+
+        def evac(eng_copy, mh, t, sg0=0, nsg=16):
+            eng_copy(
+                out=d2in[t // 8][:, sg0 : sg0 + nsg, t % 8, 8 * mh : 8 * mh + 8, :],
+                in_=acc[t][:].rearrange("p (sg m j) -> p sg m j", m=8, j=4),
+            )
+
+        def quant_d2(q, cod, sca, sg0, nsg):
+            nc.vector.quantize_mx(
+                out=cod[:, sg0 : sg0 + nsg, :].rearrange("p sg w -> p (sg w)").bitcast(FP8X4),
+                scales=sca[:, sg0 : sg0 + nsg, :].rearrange("p sg w -> p (sg w)"),
+                in_=d2in[q][:, sg0 : sg0 + nsg].rearrange("p sg t m j -> p (sg t m j)"),
+            )
+
+        def new_codes():
+            cod = d2q.tile([P, 16, 128], U32, tag="d2c", name="d2c", align_bytes=64)
+            sca = d2q.tile([P, 16, 128], U8, tag="d2s", name="d2s", align_bytes=64)
+            return cod, sca
+
+        def pass2(term, cod, sca, sg):
+            nc.tensor.matmul_mx(
+                out=term[:],
+                lhsT=cod[:, sg, :].bitcast(FP8X4),
+                lhsT_scale=sca[:, sg, :],
+                rhs=g2c[:, sg, :].bitcast(FP8X4),
+                rhs_scale=g2s[:, sg, :],
+                start=(sg == 0),
+                stop=(sg == 15),
+            )
+
+        def finish(q, term):
+            res = d2q.tile([P, 128], F32, tag="res", name="res")
+            nc.vector.tensor_tensor(out=res[:], in0=base[:, q, :], in1=term[:], op=SUB)
+            nc.sync.dma_start(out=outv[128 * q : 128 * q + 128, :], in_=res[:])
+
+        def second_core(q, cod, sca):
+            term = psum.tile([P, 128], F32, tag="bank", name="term")
+            for sg in range(16):
+                pass2(term, cod, sca, sg)
+            finish(q, term)
+
         g1raw0 = load_g1(0)
-        r00 = load_d1(0, 0)
-        r01 = load_d1(0, 1)
-        r10 = load_d1(1, 0)
-        prep_g1(0, g1raw0)
-        units(0, 0, r00)
-        r11 = load_d1(1, 1)
-        units(0, 1, r01)
+        r0 = load_d1(0, 0, 1)
+        r1 = load_d1(0, 1, 1)
+        r2 = load_d1(1, 0, 1)
+        g1grp0 = s8.tile([P, 2, 16, 8, 4, 4], BF16, tag="s8", name="g1grp0", align_bytes=64)
+        g1_copy(g1grp0, g1raw0, 0)
+        g1_copy(g1grp0, g1raw0, 1)
+        g1_quant(g1grp0, 0)
+        units(r0, 0, 0, 0, 64, 4)
+        r3 = load_d1(1, 1, 2)
+        units(r1, 0, 64, 0, 64, 4)
         g1raw1 = load_g1(1)
         g2raw = raw16.tile([P, 64, 128], BF16, tag="raw16", name="g2raw")
         nc.sync.dma_start(out=g2raw[:], in_=g2.rearrange("s (h l) a o -> (s h) l (a o)", h=2))
         nc.sync.dma_start(out=xt[:], in_=x_l.rearrange("b (r j) -> (b r) j", j=128).rearrange("(q p) j -> p q j", p=P))
         nc.sync.dma_start(out=mt[:], in_=mv.rearrange("b (r j) -> (b r) j", j=128).rearrange("(q p) j -> p q j", p=P))
         nc.sync.dma_start(out=bt[:], in_=bias.rearrange("(h p j) -> p h j", p=P, j=128))
-        for tq in range(8):
+        quant_d1(0, 0)
+        quant_d1(1, 0)
+        for t in range(8):
+            new_acc(t)
+            pass1(0, t, 0)
+        units(r2, 1, 0, 0, 64, 5)
+        units(r3, 1, 64, 0, 32, 5)
+
+        def last_unit(tq):
+            unit(nc.vector.tensor_copy, r3, 1, 96, 32, 32, tq)
+
+        last_unit(0)
+        quant_d1(0, 1)
+        last_unit(1)
+        last_unit(2)
+        quant_d1(1, 1)
+        quant_d1(2, 0)
+        quant_d1(2, 1)
+        for tq in range(3, 8):
+            last_unit(tq)
             quant_d1(tq, 0)
-        units(1, 0, r10)
-        units(1, 1, r11)
+            quant_d1(tq, 1)
 
-        d2in = {}
-
-        def first_core(mh, t):
-            q, tl = t // 8, t % 8
-            acc = ps1.tile([P, 512], F32, tag="ps1", name="acc")
-            for c in range(2):
-                nc.tensor.matmul_mx(
-                    out=acc[:],
-                    lhsT=d1c[:, t // 4, c, 128 * (t % 4) : 128 * (t % 4) + 128].bitcast(FP8X4),
-                    lhsT_scale=d1s[:, t // 4, c, 128 * (t % 4) : 128 * (t % 4) + 128],
-                    rhs=g1c[:, mh, c, :].bitcast(FP8X4),
-                    rhs_scale=g1s[:, mh, c, :],
-                    start=(c == 0),
-                    stop=(c == 1),
-                )
-            dst = d2in[q][:, :, tl, 8 * mh : 8 * mh + 8, :]
-            src = acc[:].rearrange("p (sg m j) -> p sg m j", m=8, j=4)
-            if t % 4 == 3:
-                nc.vector.tensor_copy(out=dst, in_=src)
-            else:
-                nc.scalar.copy(out=dst, in_=src)
-
+        g1grp1 = s8.tile([P, 2, 16, 8, 4, 4], BF16, tag="s8", name="g1grp1", align_bytes=64)
+        g2in = None
+        bunch = 0
         for t in range(32):
-            if t % 4 == 0:
-                quant_d1(t // 4, 1)
             if t % 8 == 0:
                 d2in[t // 8] = big16.tile(
                     [P, 16, 8, 16, 4], BF16, tag="big16", name="d2in%d" % (t // 8), align_bytes=64
                 )
-            first_core(0, t)
-
-        prep_g1(1, g1raw1)
-        nc.vector.tensor_tensor(out=base[:], in0=xt[:], in1=mt[:], op=ADD)
-        for b in range(2):
-            nc.vector.tensor_tensor(out=base[:, 2 * b : 2 * b + 2, :], in0=base[:, 2 * b : 2 * b + 2, :], in1=bt[:], op=ADD)
-
-        g2in = big16.tile([P, 16, 2, 64, 4], BF16, tag="big16", name="g2in", align_bytes=64)
-        for grp8 in range(8):
-            tp = pst.tile([P, 8, 128], BF16, tag="pst", name="tp")
-            for g in range(8):
-                nc.tensor.transpose(tp[:, g, :], g2raw[:, 8 * grp8 + g, :], ident[:])
-            for jh in range(2):
-                nc.scalar.copy(
-                    out=g2in[:, :, jh, 8 * grp8 : 8 * grp8 + 8, :],
-                    in_=tp[:].rearrange("p g (sg j h) -> p h sg g j", j=4, h=2)[:, jh],
-                )
+            if t >= 8:
+                new_acc(t)
+                pass1(0, t, 0)
+            pass1(0, t, 1)
+            evac(nc.scalar.copy, 0, t)
+            if t in (20, 23, 26, 29):
+                if g2in is None:
+                    g2in = big16.tile([P, 16, 2, 64, 4], BF16, tag="big16", name="g2in", align_bytes=64)
+                tps = []
+                for half in range(2):
+                    tp = psum.tile([P, 8, 128], BF16, tag="bank", name="tp")
+                    for g in range(8):
+                        nc.tensor.transpose(tp[:, g, :], g2raw[:, 16 * bunch + 8 * half + g, :], ident[:])
+                    tps.append(tp)
+                for half in range(2):
+                    l0 = 16 * bunch + 8 * half
+                    for jh in range(2):
+                        nc.vector.tensor_copy(
+                            out=g2in[:, :, jh, l0 : l0 + 8, :],
+                            in_=tps[half][:].rearrange("p g (sg j h) -> p h sg g j", j=4, h=2)[:, jh],
+                        )
+                if bunch < 2:
+                    g1_copy(g1grp1, g1raw1, bunch)
+                if bunch == 2:
+                    g1_quant(g1grp1, 1)
+                bunch += 1
         for h in range(2):
             nc.vector.quantize_mx(
                 out=g2c[:, 8 * h : 8 * h + 8, :].rearrange("p sg w -> p (sg w)").bitcast(FP8X4),
                 scales=g2s[:, 8 * h : 8 * h + 8, :].rearrange("p sg w -> p (sg w)"),
                 in_=g2in[:, 8 * h : 8 * h + 8].rearrange("p sg h l j -> p (sg h l j)"),
             )
+        nc.vector.tensor_tensor(out=base[:], in0=xt[:], in1=mt[:], op=ADD)
+        for b in range(2):
+            nc.vector.tensor_tensor(out=base[:, 2 * b : 2 * b + 2, :], in0=base[:, 2 * b : 2 * b + 2, :], in1=bt[:], op=ADD)
 
-        def second_core(q):
-            cod = d2q.tile([P, 16, 128], U32, tag="d2c", name="d2c", align_bytes=64)
-            sca = d2q.tile([P, 16, 128], U8, tag="d2s", name="d2s", align_bytes=64)
-            for h in range(2):
-                nc.vector.quantize_mx(
-                    out=cod[:, 8 * h : 8 * h + 8, :].rearrange("p sg w -> p (sg w)").bitcast(FP8X4),
-                    scales=sca[:, 8 * h : 8 * h + 8, :].rearrange("p sg w -> p (sg w)"),
-                    in_=d2in[q][:, 8 * h : 8 * h + 8].rearrange("p sg t m j -> p (sg t m j)"),
-                )
-            term = ps2.tile([P, 128], F32, tag="ps2", name="term")
-            for sg in range(16):
-                nc.tensor.matmul_mx(
-                    out=term[:],
-                    lhsT=cod[:, sg, :].bitcast(FP8X4),
-                    lhsT_scale=sca[:, sg, :],
-                    rhs=g2c[:, sg, :].bitcast(FP8X4),
-                    rhs_scale=g2s[:, sg, :],
-                    start=(sg == 0),
-                    stop=(sg == 15),
-                )
-            res = d2q.tile([P, 128], F32, tag="res", name="res")
-            nc.vector.tensor_tensor(out=res[:], in0=base[:, q, :], in1=term[:], op=SUB)
-            nc.sync.dma_start(out=outv[128 * q : 128 * q + 128, :], in_=res[:])
+        codes = {}
+        for t in range(24):
+            new_acc(t)
+            pass1(1, t, 0)
+            pass1(1, t, 1)
+            evac(nc.vector.tensor_copy if t % 4 == 1 else nc.scalar.copy, 1, t)
+            if t % 8 == 7:
+                codes[t // 8] = new_codes()
+                quant_d2(t // 8, codes[t // 8][0], codes[t // 8][1], 0, 8)
+                quant_d2(t // 8, codes[t // 8][0], codes[t // 8][1], 8, 8)
+            if t in (13, 21):
+                second_core(t // 8 - 1, codes[t // 8 - 1][0], codes[t // 8 - 1][1])
 
-        for t in range(32):
-            first_core(1, t)
-            if t % 8 == 3 and t >= 11:
-                second_core(t // 8 - 1)
-        second_core(3)
+        for t in range(24, 32):
+            new_acc(t, 256)
+            pass1(1, t, 0, 0, 256)
+            pass1(1, t, 1, 0, 256)
+            evac(nc.scalar.copy, 1, t, 0, 8)
+            if t == 27:
+                second_core(2, codes[2][0], codes[2][1])
+        cod3, sca3 = new_codes()
+        quant_d2(3, cod3, sca3, 0, 8)
+        for t in range(24, 32):
+            new_acc(t, 256)
+            pass1(1, t, 0, 256, 256)
+            pass1(1, t, 1, 256, 256)
+            evac(nc.vector.tensor_copy if t % 2 == 0 else nc.scalar.copy, 1, t, 8, 8)
+        term3 = psum.tile([P, 128], F32, tag="bank", name="term")
+        for sg in range(8):
+            pass2(term3, cod3, sca3, sg)
+        quant_d2(3, cod3, sca3, 8, 4)
+        quant_d2(3, cod3, sca3, 12, 4)
+        for sg in range(8, 16):
+            pass2(term3, cod3, sca3, sg)
+        finish(3, term3)

@@ -160,15 +160,15 @@ def tile_ttsolver_pa_kernel(tc, d1, g1, g2, x_l, mv, bias, out):
                 pass2(term, cod, sca, sg)
             finish(q, term)
 
-        g1raw0 = load_g1(0)
         r0 = load_d1(0, 0, 1)
+        g1raw0 = load_g1(0)
         r1 = load_d1(0, 1, 1)
         r2 = load_d1(1, 0, 1)
+        units(r0, 0, 0, 0, 64, 2)
         g1grp0 = s8.tile([P, 2, 16, 8, 4, 4], BF16, tag="s8", name="g1grp0", align_bytes=64)
         g1_copy(g1grp0, g1raw0, 0)
         g1_copy(g1grp0, g1raw0, 1)
         g1_quant(g1grp0, 0)
-        units(r0, 0, 0, 0, 64, 4)
         r3 = load_d1(1, 1, 2)
         units(r1, 0, 64, 0, 64, 4)
         g1raw1 = load_g1(1)
@@ -182,27 +182,39 @@ def tile_ttsolver_pa_kernel(tc, d1, g1, g2, x_l, mv, bias, out):
         for t in range(8):
             new_acc(t)
             pass1(0, t, 0)
-        units(r2, 1, 0, 0, 64, 5)
-        units(r3, 1, 64, 0, 32, 5)
+        quant_d1(2, 0)
+        quant_d1(3, 0)
+        units(r2, 1, 0, 0, 64, 4)
+        units(r3, 1, 64, 0, 32, 6)
 
         def last_unit(tq):
             unit(nc.vector.tensor_copy, r3, 1, 96, 32, 32, tq)
 
+        def quant_d1_part(t_lo, t_n):
+            nc.vector.quantize_mx(
+                out=d1c[:, 0, 1, 128 * t_lo : 128 * (t_lo + t_n)].bitcast(FP8X4),
+                scales=d1s[:, 0, 1, 128 * t_lo : 128 * (t_lo + t_n)],
+                in_=grouped[0][:, 0, 1, t_lo : t_lo + t_n].rearrange("p t a j -> p (t a j)"),
+            )
+
         last_unit(0)
-        quant_d1(0, 1)
+        quant_d1_part(0, 1)
+        quant_d1_part(1, 1)
+        quant_d1_part(2, 2)
         last_unit(1)
         last_unit(2)
         quant_d1(1, 1)
-        quant_d1(2, 0)
         quant_d1(2, 1)
-        for tq in range(3, 8):
-            last_unit(tq)
+        last_unit(3)
+        last_unit(4)
+        quant_d1(3, 1)
+        for tq in range(4, 8):
+            if tq < 7:
+                last_unit(tq + 1)
             quant_d1(tq, 0)
             quant_d1(tq, 1)
 
         g1grp1 = s8.tile([P, 2, 16, 8, 4, 4], BF16, tag="s8", name="g1grp1", align_bytes=64)
-        g2in = None
-        bunch = 0
         for t in range(32):
             if t % 8 == 0:
                 d2in[t // 8] = big16.tile(
@@ -212,10 +224,28 @@ def tile_ttsolver_pa_kernel(tc, d1, g1, g2, x_l, mv, bias, out):
                 new_acc(t)
                 pass1(0, t, 0)
             pass1(0, t, 1)
-            evac(nc.scalar.copy, 0, t)
-            if t in (20, 23, 26, 29):
-                if g2in is None:
-                    g2in = big16.tile([P, 16, 2, 64, 4], BF16, tag="big16", name="g2in", align_bytes=64)
+            evac(nc.vector.tensor_copy if t in (20, 23, 26, 29) else nc.scalar.copy, 0, t)
+            if t in (20, 23):
+                g1_copy(g1grp1, g1raw1, (t - 20) // 3)
+            if t == 26:
+                g1_quant(g1grp1, 1)
+        nc.vector.tensor_tensor(out=base[:], in0=xt[:], in1=mt[:], op=ADD)
+        for b in range(2):
+            nc.vector.tensor_tensor(out=base[:, 2 * b : 2 * b + 2, :], in0=base[:, 2 * b : 2 * b + 2, :], in1=bt[:], op=ADD)
+
+        g2in = big16.tile([P, 16, 2, 64, 4], BF16, tag="big16", name="g2in", align_bytes=64)
+        codes = {}
+        for t in range(24):
+            new_acc(t)
+            pass1(1, t, 0)
+            pass1(1, t, 1)
+            evac(nc.vector.tensor_copy if t % 8 == 3 else nc.scalar.copy, 1, t)
+            if t % 8 == 7:
+                codes[t // 8] = new_codes()
+                quant_d2(t // 8, codes[t // 8][0], codes[t // 8][1], 0, 8)
+                quant_d2(t // 8, codes[t // 8][0], codes[t // 8][1], 8, 8)
+            if t in (1, 4, 8, 11):
+                bunch = (1, 4, 8, 11).index(t)
                 tps = []
                 for half in range(2):
                     tp = psum.tile([P, 8, 128], BF16, tag="bank", name="tp")
@@ -224,38 +254,21 @@ def tile_ttsolver_pa_kernel(tc, d1, g1, g2, x_l, mv, bias, out):
                     tps.append(tp)
                 for half in range(2):
                     l0 = 16 * bunch + 8 * half
+                    cp = nc.vector.tensor_copy if half == 0 else nc.scalar.copy
                     for jh in range(2):
-                        nc.vector.tensor_copy(
+                        cp(
                             out=g2in[:, :, jh, l0 : l0 + 8, :],
                             in_=tps[half][:].rearrange("p g (sg j h) -> p h sg g j", j=4, h=2)[:, jh],
                         )
-                if bunch < 2:
-                    g1_copy(g1grp1, g1raw1, bunch)
-                if bunch == 2:
-                    g1_quant(g1grp1, 1)
-                bunch += 1
-        for h in range(2):
-            nc.vector.quantize_mx(
-                out=g2c[:, 8 * h : 8 * h + 8, :].rearrange("p sg w -> p (sg w)").bitcast(FP8X4),
-                scales=g2s[:, 8 * h : 8 * h + 8, :].rearrange("p sg w -> p (sg w)"),
-                in_=g2in[:, 8 * h : 8 * h + 8].rearrange("p sg h l j -> p (sg h l j)"),
-            )
-        nc.vector.tensor_tensor(out=base[:], in0=xt[:], in1=mt[:], op=ADD)
-        for b in range(2):
-            nc.vector.tensor_tensor(out=base[:, 2 * b : 2 * b + 2, :], in0=base[:, 2 * b : 2 * b + 2, :], in1=bt[:], op=ADD)
-
-        codes = {}
-        for t in range(24):
-            new_acc(t)
-            pass1(1, t, 0)
-            pass1(1, t, 1)
-            evac(nc.vector.tensor_copy if t % 4 == 1 else nc.scalar.copy, 1, t)
-            if t % 8 == 7:
-                codes[t // 8] = new_codes()
-                quant_d2(t // 8, codes[t // 8][0], codes[t // 8][1], 0, 8)
-                quant_d2(t // 8, codes[t // 8][0], codes[t // 8][1], 8, 8)
-            if t in (13, 21):
-                second_core(t // 8 - 1, codes[t // 8 - 1][0], codes[t // 8 - 1][1])
+            if t == 11:
+                for h in range(2):
+                    nc.vector.quantize_mx(
+                        out=g2c[:, 8 * h : 8 * h + 8, :].rearrange("p sg w -> p (sg w)").bitcast(FP8X4),
+                        scales=g2s[:, 8 * h : 8 * h + 8, :].rearrange("p sg w -> p (sg w)"),
+                        in_=g2in[:, 8 * h : 8 * h + 8].rearrange("p sg h l j -> p (sg h l j)"),
+                    )
+            if t in (17, 22):
+                second_core((t - 17) // 5, codes[(t - 17) // 5][0], codes[(t - 17) // 5][1])
 
         for t in range(24, 32):
             new_acc(t, 256)

@@ -170,7 +170,7 @@ def tile_ttsolver_pa_kernel(tc, d1, g1, g2, x_l, mv, bias, out):
         g1_copy(g1grp0, g1raw0, 1)
         g1_quant(g1grp0, 0)
         r3 = load_d1(1, 1, 2)
-        units(r1, 0, 64, 0, 64, 4)
+        units(r1, 0, 64, 0, 64, 3)
         g1raw1 = load_g1(1)
         g2raw = raw16.tile([P, 64, 128], BF16, tag="raw16", name="g2raw")
         nc.sync.dma_start(out=g2raw[:], in_=g2.rearrange("s (h l) a o -> (s h) l (a o)", h=2))
@@ -184,8 +184,8 @@ def tile_ttsolver_pa_kernel(tc, d1, g1, g2, x_l, mv, bias, out):
             pass1(0, t, 0)
         quant_d1(2, 0)
         quant_d1(3, 0)
-        units(r2, 1, 0, 0, 64, 4)
-        units(r3, 1, 64, 0, 32, 6)
+        units(r2, 1, 0, 0, 64, 3)
+        units(r3, 1, 64, 0, 32, 4)
 
         def last_unit(tq):
             unit(nc.vector.tensor_copy, r3, 1, 96, 32, 32, tq)

@@ -170,7 +170,7 @@ def tile_ttsolver_pa_kernel(tc, d1, g1, g2, x_l, mv, bias, out):
         g1_copy(g1grp0, g1raw0, 1)
         g1_quant(g1grp0, 0)
         r3 = load_d1(1, 1, 2)
-        units(r1, 0, 64, 0, 64, 3)
+        units(r1, 0, 64, 0, 64, 4)
         g1raw1 = load_g1(1)
         g2raw = raw16.tile([P, 64, 128], BF16, tag="raw16", name="g2raw")
         nc.sync.dma_start(out=g2raw[:], in_=g2.rearrange("s (h l) a o -> (s h) l (a o)", h=2))
@@ -184,8 +184,8 @@ def tile_ttsolver_pa_kernel(tc, d1, g1, g2, x_l, mv, bias, out):
             pass1(0, t, 0)
         quant_d1(2, 0)
         quant_d1(3, 0)
-        units(r2, 1, 0, 0, 64, 3)
-        units(r3, 1, 64, 0, 32, 4)
+        units(r2, 1, 0, 0, 64, 4)
+        units(r3, 1, 64, 0, 32, 6)
 
         def last_unit(tq):
             unit(nc.vector.tensor_copy, r3, 1, 96, 32, 32, tq)
@@ -224,10 +224,10 @@ def tile_ttsolver_pa_kernel(tc, d1, g1, g2, x_l, mv, bias, out):
                 new_acc(t)
                 pass1(0, t, 0)
             pass1(0, t, 1)
-            evac(nc.vector.tensor_copy if t in (20, 23, 26, 29) else nc.scalar.copy, 0, t)
-            if t in (20, 23):
-                g1_copy(g1grp1, g1raw1, (t - 20) // 3)
-            if t == 26:
+            evac(nc.vector.tensor_copy if (t >= 17 and t % 2 == 1) else nc.scalar.copy, 0, t)
+            if t in (17, 19):
+                g1_copy(g1grp1, g1raw1, (t - 17) // 2)
+            if t == 21:
                 g1_quant(g1grp1, 1)
         nc.vector.tensor_tensor(out=base[:], in0=xt[:], in1=mt[:], op=ADD)
         for b in range(2):
@@ -239,13 +239,13 @@ def tile_ttsolver_pa_kernel(tc, d1, g1, g2, x_l, mv, bias, out):
             new_acc(t)
             pass1(1, t, 0)
             pass1(1, t, 1)
-            evac(nc.vector.tensor_copy if t % 8 == 3 else nc.scalar.copy, 1, t)
+            evac(nc.vector.tensor_copy if t % 8 == 5 else nc.scalar.copy, 1, t)
             if t % 8 == 7:
                 codes[t // 8] = new_codes()
                 quant_d2(t // 8, codes[t // 8][0], codes[t // 8][1], 0, 8)
                 quant_d2(t // 8, codes[t // 8][0], codes[t // 8][1], 8, 8)
-            if t in (1, 4, 8, 11):
-                bunch = (1, 4, 8, 11).index(t)
+            if t % 3 == 0 and t < 12:
+                bunch = t // 3
                 tps = []
                 for half in range(2):
                     tp = psum.tile([P, 8, 128], BF16, tag="bank", name="tp")
@@ -260,15 +260,15 @@ def tile_ttsolver_pa_kernel(tc, d1, g1, g2, x_l, mv, bias, out):
                             out=g2in[:, :, jh, l0 : l0 + 8, :],
                             in_=tps[half][:].rearrange("p g (sg j h) -> p h sg g j", j=4, h=2)[:, jh],
                         )
-            if t == 11:
+            if t == 9:
                 for h in range(2):
                     nc.vector.quantize_mx(
                         out=g2c[:, 8 * h : 8 * h + 8, :].rearrange("p sg w -> p (sg w)").bitcast(FP8X4),
                         scales=g2s[:, 8 * h : 8 * h + 8, :].rearrange("p sg w -> p (sg w)"),
                         in_=g2in[:, 8 * h : 8 * h + 8].rearrange("p sg h l j -> p (sg h l j)"),
                     )
-            if t in (17, 22):
-                second_core((t - 17) // 5, codes[(t - 17) // 5][0], codes[(t - 17) // 5][1])
+            if t in (19, 23):
+                second_core((t - 19) // 4, codes[(t - 19) // 4][0], codes[(t - 19) // 4][1])
 
         for t in range(24, 32):
             new_acc(t, 256)

@@ -11,284 +11,264 @@ U32 = mybir.dt.uint32
 U8 = mybir.dt.uint8
 FP8X4 = mybir.dt.float8_e4m3fn_x4
 ADD = mybir.AluOpType.add
-SUB = mybir.AluOpType.subtract
+SUBTRACT = mybir.AluOpType.subtract
+
 P = 128
+PACK = 4
+N_T = 32
+N_SG = 16
+M_HALF = 8
+T_GROUP = 4
+N_GROUPS = N_T // T_GROUP
+T_BLOCK = 8
+PSUM_BANKS = 8
+SG_PER_QUANT = 4
+
+D1_CHUNKS = ((0, 0, 64, 2), (0, 64, 64, 4), (1, 0, 64, 4), (1, 64, 32, 6), (1, 96, 32, 8))
+RAW_SLOTS = 3
+
+EARLY_C0_GROUPS = 4
+VECTOR_HELPS_FROM = 17
+VECTOR_HELPS_AT = 5
+SECOND_CORE_FIRST_STEP = 19
+SECOND_CORE_STEP = 4
 
 
 def tile_ttsolver_pa_kernel(tc, d1, g1, g2, x_l, mv, bias, out):
     nc = tc.nc
     with ExitStack() as ctx:
-        raw16 = ctx.enter_context(tc.tile_pool(name="raw16", bufs=3))
-        big16 = ctx.enter_context(tc.tile_pool(name="big16", bufs=5))
-        s8 = ctx.enter_context(tc.tile_pool(name="s8", bufs=2))
+        raw_pool = ctx.enter_context(tc.tile_pool(name="raw", bufs=RAW_SLOTS))
+        big_pool = ctx.enter_context(tc.tile_pool(name="big", bufs=5))
+        g1_pool = ctx.enter_context(tc.tile_pool(name="g1", bufs=2))
         keep = ctx.enter_context(tc.tile_pool(name="keep", bufs=1))
-        d2q = ctx.enter_context(tc.tile_pool(name="d2q", bufs=2))
-        psum = ctx.enter_context(tc.psum_pool(name="psum", bufs=8))
+        block_pool = ctx.enter_context(tc.tile_pool(name="block", bufs=2))
+        psum = ctx.enter_context(tc.psum_pool(name="psum", bufs=PSUM_BANKS))
         ctx.enter_context(tc.manual_schedule())
 
-        d1c = keep.tile([P, 8, 2, 512], U32, align_bytes=64)
-        d1s = keep.tile([P, 8, 2, 512], U8, align_bytes=64)
-        g1c = keep.tile([P, 2, 2, 512], U32, align_bytes=64)
-        g1s = keep.tile([P, 2, 2, 512], U8, align_bytes=64)
-        g2c = keep.tile([P, 16, 128], U32, align_bytes=64)
-        g2s = keep.tile([P, 16, 128], U8, align_bytes=64)
-        ident = keep.tile([P, P], BF16)
-        xt = keep.tile([P, 4, 128], BF16)
-        mt = keep.tile([P, 4, 128], BF16)
-        bt = keep.tile([P, 2, 128], BF16)
-        base = keep.tile([P, 4, 128], F32)
+        d1_words = keep.tile([P, N_GROUPS, 2, T_GROUP * P], U32, align_bytes=64)
+        d1_scales = keep.tile([P, N_GROUPS, 2, T_GROUP * P], U8, align_bytes=64)
+        g1_words = keep.tile([P, 2, 2, 512], U32, align_bytes=64)
+        g1_scales = keep.tile([P, 2, 2, 512], U8, align_bytes=64)
+        g2_words = keep.tile([P, N_SG, P], U32, align_bytes=64)
+        g2_scales = keep.tile([P, N_SG, P], U8, align_bytes=64)
+        identity = keep.tile([P, P], BF16)
+        x_rows = keep.tile([P, 4, P], BF16)
+        mv_rows = keep.tile([P, 4, P], BF16)
+        bias_rows = keep.tile([P, 2, P], BF16)
+        base = keep.tile([P, 4, P], F32)
 
-        make_identity(nc, ident[:])
+        make_identity(nc, identity[:])
 
-        d1v = d1.rearrange("r (n a) t -> (r n) (a t)", n=16)
-        outv = out.rearrange("b (r j) -> (b r) j", j=128)
+        d1_rows = d1.rearrange("r (n a) t -> (r n) (a t)", n=16)
+        out_rows = out.rearrange("b (r j) -> (b r) j", j=P)
 
-        def load_g1(mh):
-            t_ = s8.tile([P, 2, 8, 256], BF16, tag="s8", name="g1raw%d" % mh, align_bytes=64)
+        def load_g1(half):
+            raw = g1_pool.tile([P, 2, M_HALF, PACK * 64], BF16, tag="g1", name="g1_raw%d" % half, align_bytes=64)
             for c in range(2):
                 for nh in range(4):
                     nc.sync.dma_start(
-                        out=t_[nh:P:4, c, :, :],
-                        in_=g1[32 * c : 32 * c + 32, 8 * mh : 8 * mh + 8, 4 * nh : 4 * nh + 4, :].rearrange(
-                            "r m n s -> r m (n s)"
-                        ),
+                        out=raw[nh:P:4, c, :, :],
+                        in_=g1[
+                            32 * c : 32 * c + 32, M_HALF * half : M_HALF * (half + 1), PACK * nh : PACK * (nh + 1), :
+                        ].rearrange("r m n s -> r m (n s)"),
                     )
-            return t_
+            return raw
 
-        def g1_copy(grp, raw, c):
+        def new_g1_grouped(half):
+            return g1_pool.tile(
+                [P, 2, N_SG, M_HALF, PACK, PACK], BF16, tag="g1", name="g1_grouped%d" % half, align_bytes=64
+            )
+
+        def regroup_g1(grouped, raw, c):
             nc.vector.tensor_copy(
-                out=grp[:, c].rearrange("p sg m j n -> p m sg n j"),
-                in_=raw[:, c].rearrange("p m (n sg j) -> p m sg n j", n=4, j=4),
+                out=grouped[:, c].rearrange("p sg m si ni -> p m sg ni si"),
+                in_=raw[:, c].rearrange("p m (ni sg si) -> p m sg ni si", ni=PACK, si=PACK),
             )
 
-        def g1_quant(grp, mh):
+        def quantise_g1(grouped, half):
             nc.vector.quantize_mx(
-                out=g1c[:, mh].rearrange("p c w -> p (c w)").bitcast(FP8X4),
-                scales=g1s[:, mh].rearrange("p c w -> p (c w)"),
-                in_=grp[:].rearrange("p c sg m j n -> p (c sg m j n)"),
+                out=g1_words[:, half].rearrange("p c w -> p (c w)").bitcast(FP8X4),
+                scales=g1_scales[:, half].rearrange("p c w -> p (c w)"),
+                in_=grouped[:].rearrange("p c sg m si ni -> p (c sg m si ni)"),
             )
 
-        def load_d1(c, ah, pieces):
-            t_ = raw16.tile([P, 4, 2048], BF16, tag="raw16", name="d1raw%d%d" % (c, ah))
-            w = 2048 // pieces
-            for i in range(pieces):
-                nc.sync.dma_start(
-                    out=t_[:, :, w * i : w * i + w],
-                    in_=d1v[512 * c : 512 * c + 512, 2048 * ah + w * i : 2048 * ah + w * i + w].rearrange(
-                        "(p j) w -> p j w", j=4
-                    ),
-                )
-            return t_
+        def load_d1(chunk):
+            c, a0, n_a = chunk[0], chunk[1], chunk[2]
+            raw = raw_pool.tile([P, PACK, n_a * N_T], BF16, tag="raw", name="d1_raw")
+            nc.sync.dma_start(
+                out=raw[:],
+                in_=d1_rows[512 * c : 512 * (c + 1), a0 * N_T : (a0 + n_a) * N_T].rearrange(
+                    "(p ni) w -> p ni w", ni=PACK
+                ),
+            )
+            return raw
 
-        grouped = [
-            big16.tile([P, 2, 2, 4, 128, 4], BF16, tag="big16", name="d1grp%d" % q, align_bytes=64) for q in range(4)
+        d1_grouped = [
+            big_pool.tile([P, 2, 2, T_GROUP, P, PACK], BF16, tag="big", name="d1_grouped%d" % i, align_bytes=64)
+            for i in range(N_GROUPS // 2)
         ]
 
-        def unit(eng_copy, raw, c, a_dst, a_src, a_len, tq):
-            eng_copy(
-                out=grouped[tq // 2][:, tq % 2, c, :, a_dst : a_dst + a_len, :].rearrange("p t a j -> p a j t"),
-                in_=raw[:].rearrange("p j (a t) -> p a j t", t=32)[:, a_src : a_src + a_len, :, 4 * tq : 4 * tq + 4],
+        def regroup_d1(copy, raw, chunk, group):
+            c, a0, n_a = chunk[0], chunk[1], chunk[2]
+            copy(
+                out=d1_grouped[group // 2][:, group % 2, c, :, a0 : a0 + n_a, :].rearrange("p t a ni -> p a ni t"),
+                in_=raw[:].rearrange("p ni (a t) -> p a ni t", t=N_T)[:, :, :, T_GROUP * group : T_GROUP * (group + 1)],
             )
 
-        def units(raw, c, a_dst, a_src, a_len, n_vector):
-            for tq in range(n_vector):
-                unit(nc.vector.tensor_copy, raw, c, a_dst, a_src, a_len, tq)
-            for tq in range(n_vector, 8):
-                unit(nc.scalar.copy, raw, c, a_dst, a_src, a_len, tq)
+        def regroup_d1_chunk(raw, chunk):
+            for group in range(N_GROUPS):
+                regroup_d1(nc.vector.tensor_copy if group < chunk[3] else nc.scalar.copy, raw, chunk, group)
 
-        def quant_d1(tq, c):
+        def quantise_d1(group, c):
             nc.vector.quantize_mx(
-                out=d1c[:, tq, c, :].bitcast(FP8X4),
-                scales=d1s[:, tq, c, :],
-                in_=grouped[tq // 2][:, tq % 2, c].rearrange("p t a j -> p (t a j)"),
+                out=d1_words[:, group, c, :].bitcast(FP8X4),
+                scales=d1_scales[:, group, c, :],
+                in_=d1_grouped[group // 2][:, group % 2, c].rearrange("p t a ni -> p (t a ni)"),
             )
 
-        acc = {}
-        d2in = {}
+        sums = {}
+        d2_blocks = {}
 
-        def pass1(mh, t, c, lo=0, n=512):
+        def first_core_pass(half, t, c):
+            if c == 0:
+                sums[t] = psum.tile([P, 512], F32, tag="bank", name="sums")
+            columns = slice(P * (t % T_GROUP), P * (t % T_GROUP + 1))
             nc.tensor.matmul_mx(
-                out=acc[t][:],
-                lhsT=d1c[:, t // 4, c, 128 * (t % 4) : 128 * (t % 4) + 128].bitcast(FP8X4),
-                lhsT_scale=d1s[:, t // 4, c, 128 * (t % 4) : 128 * (t % 4) + 128],
-                rhs=g1c[:, mh, c, lo : lo + n].bitcast(FP8X4),
-                rhs_scale=g1s[:, mh, c, lo : lo + n],
+                out=sums[t][:],
+                lhsT=d1_words[:, t // T_GROUP, c, columns].bitcast(FP8X4),
+                lhsT_scale=d1_scales[:, t // T_GROUP, c, columns],
+                rhs=g1_words[:, half, c, :].bitcast(FP8X4),
+                rhs_scale=g1_scales[:, half, c, :],
                 start=(c == 0),
                 stop=(c == 1),
             )
 
-        def new_acc(t, n=512):
-            acc[t] = psum.tile([P, n], F32, tag="bank", name="acc")
-
-        def evac(eng_copy, mh, t, sg0=0, nsg=16):
-            eng_copy(
-                out=d2in[t // 8][:, sg0 : sg0 + nsg, t % 8, 8 * mh : 8 * mh + 8, :],
-                in_=acc[t][:].rearrange("p (sg m j) -> p sg m j", m=8, j=4),
+        def round_d2(copy, half, t):
+            copy(
+                out=d2_blocks[t // T_BLOCK][:, :, t % T_BLOCK, M_HALF * half : M_HALF * (half + 1), :],
+                in_=sums[t][:].rearrange("p (sg m si) -> p sg m si", m=M_HALF, si=PACK),
             )
 
-        def quant_d2(q, cod, sca, sg0, nsg):
-            nc.vector.quantize_mx(
-                out=cod[:, sg0 : sg0 + nsg, :].rearrange("p sg w -> p (sg w)").bitcast(FP8X4),
-                scales=sca[:, sg0 : sg0 + nsg, :].rearrange("p sg w -> p (sg w)"),
-                in_=d2in[q][:, sg0 : sg0 + nsg].rearrange("p sg t m j -> p (sg t m j)"),
-            )
+        block_codes = {}
 
-        def new_codes():
-            cod = d2q.tile([P, 16, 128], U32, tag="d2c", name="d2c", align_bytes=64)
-            sca = d2q.tile([P, 16, 128], U8, tag="d2s", name="d2s", align_bytes=64)
-            return cod, sca
-
-        def pass2(term, cod, sca, sg):
-            nc.tensor.matmul_mx(
-                out=term[:],
-                lhsT=cod[:, sg, :].bitcast(FP8X4),
-                lhsT_scale=sca[:, sg, :],
-                rhs=g2c[:, sg, :].bitcast(FP8X4),
-                rhs_scale=g2s[:, sg, :],
-                start=(sg == 0),
-                stop=(sg == 15),
-            )
-
-        def finish(q, term):
-            res = d2q.tile([P, 128], F32, tag="res", name="res")
-            nc.vector.tensor_tensor(out=res[:], in0=base[:, q, :], in1=term[:], op=SUB)
-            nc.sync.dma_start(out=outv[128 * q : 128 * q + 128, :], in_=res[:])
-
-        def second_core(q, cod, sca):
-            term = psum.tile([P, 128], F32, tag="bank", name="term")
-            for sg in range(16):
-                pass2(term, cod, sca, sg)
-            finish(q, term)
-
-        r0 = load_d1(0, 0, 1)
-        g1raw0 = load_g1(0)
-        r1 = load_d1(0, 1, 1)
-        r2 = load_d1(1, 0, 1)
-        units(r0, 0, 0, 0, 64, 2)
-        g1grp0 = s8.tile([P, 2, 16, 8, 4, 4], BF16, tag="s8", name="g1grp0", align_bytes=64)
-        g1_copy(g1grp0, g1raw0, 0)
-        g1_copy(g1grp0, g1raw0, 1)
-        g1_quant(g1grp0, 0)
-        r3 = load_d1(1, 1, 2)
-        units(r1, 0, 64, 0, 64, 4)
-        g1raw1 = load_g1(1)
-        g2raw = raw16.tile([P, 64, 128], BF16, tag="raw16", name="g2raw")
-        nc.sync.dma_start(out=g2raw[:], in_=g2.rearrange("s (h l) a o -> (s h) l (a o)", h=2))
-        nc.sync.dma_start(out=xt[:], in_=x_l.rearrange("b (r j) -> (b r) j", j=128).rearrange("(q p) j -> p q j", p=P))
-        nc.sync.dma_start(out=mt[:], in_=mv.rearrange("b (r j) -> (b r) j", j=128).rearrange("(q p) j -> p q j", p=P))
-        nc.sync.dma_start(out=bt[:], in_=bias.rearrange("(h p j) -> p h j", p=P, j=128))
-        quant_d1(0, 0)
-        quant_d1(1, 0)
-        for t in range(8):
-            new_acc(t)
-            pass1(0, t, 0)
-        quant_d1(2, 0)
-        quant_d1(3, 0)
-        units(r2, 1, 0, 0, 64, 4)
-        units(r3, 1, 64, 0, 32, 6)
-
-        def last_unit(tq):
-            unit(nc.vector.tensor_copy, r3, 1, 96, 32, 32, tq)
-
-        def quant_d1_part(t_lo, t_n):
-            nc.vector.quantize_mx(
-                out=d1c[:, 0, 1, 128 * t_lo : 128 * (t_lo + t_n)].bitcast(FP8X4),
-                scales=d1s[:, 0, 1, 128 * t_lo : 128 * (t_lo + t_n)],
-                in_=grouped[0][:, 0, 1, t_lo : t_lo + t_n].rearrange("p t a j -> p (t a j)"),
-            )
-
-        last_unit(0)
-        quant_d1_part(0, 1)
-        quant_d1_part(1, 1)
-        quant_d1_part(2, 2)
-        last_unit(1)
-        last_unit(2)
-        quant_d1(1, 1)
-        quant_d1(2, 1)
-        last_unit(3)
-        last_unit(4)
-        quant_d1(3, 1)
-        for tq in range(4, 8):
-            if tq < 7:
-                last_unit(tq + 1)
-            quant_d1(tq, 0)
-            quant_d1(tq, 1)
-
-        g1grp1 = s8.tile([P, 2, 16, 8, 4, 4], BF16, tag="s8", name="g1grp1", align_bytes=64)
-        for t in range(32):
-            if t % 8 == 0:
-                d2in[t // 8] = big16.tile(
-                    [P, 16, 8, 16, 4], BF16, tag="big16", name="d2in%d" % (t // 8), align_bytes=64
+        def quantise_block(q):
+            words = block_pool.tile([P, N_SG, P], U32, tag="words", name="d2_words", align_bytes=64)
+            scales = block_pool.tile([P, N_SG, P], U8, tag="scales", name="d2_scales", align_bytes=64)
+            block_codes[q] = (words, scales)
+            for sg in range(0, N_SG, SG_PER_QUANT):
+                part = slice(sg, sg + SG_PER_QUANT)
+                nc.vector.quantize_mx(
+                    out=words[:, part, :].rearrange("p sg w -> p (sg w)").bitcast(FP8X4),
+                    scales=scales[:, part, :].rearrange("p sg w -> p (sg w)"),
+                    in_=d2_blocks[q][:, part].rearrange("p sg t m si -> p (sg t m si)"),
                 )
-            if t >= 8:
-                new_acc(t)
-                pass1(0, t, 0)
-            pass1(0, t, 1)
-            evac(nc.vector.tensor_copy if (t >= 17 and t % 2 == 1) else nc.scalar.copy, 0, t)
-            if t in (17, 19):
-                g1_copy(g1grp1, g1raw1, (t - 17) // 2)
-            if t == 21:
-                g1_quant(g1grp1, 1)
-        nc.vector.tensor_tensor(out=base[:], in0=xt[:], in1=mt[:], op=ADD)
+
+        def second_core(q):
+            words, scales = block_codes[q]
+            term = psum.tile([P, P], F32, tag="bank", name="term")
+            for sg in range(N_SG):
+                nc.tensor.matmul_mx(
+                    out=term[:],
+                    lhsT=words[:, sg, :].bitcast(FP8X4),
+                    lhsT_scale=scales[:, sg, :],
+                    rhs=g2_words[:, sg, :].bitcast(FP8X4),
+                    rhs_scale=g2_scales[:, sg, :],
+                    start=(sg == 0),
+                    stop=(sg == N_SG - 1),
+                )
+            result = block_pool.tile([P, P], F32, tag="result", name="result")
+            nc.vector.tensor_tensor(out=result[:], in0=base[:, q, :], in1=term[:], op=SUBTRACT)
+            nc.sync.dma_start(out=out_rows[P * q : P * (q + 1), :], in_=result[:])
+
+        raws = {0: load_d1(D1_CHUNKS[0])}
+        g1_raw0 = load_g1(0)
+        raws[1] = load_d1(D1_CHUNKS[1])
+        raws[2] = load_d1(D1_CHUNKS[2])
+
+        regroup_d1_chunk(raws[0], D1_CHUNKS[0])
+        raws[3] = load_d1(D1_CHUNKS[3])
+        g1_grouped0 = new_g1_grouped(0)
+        regroup_g1(g1_grouped0, g1_raw0, 0)
+        regroup_g1(g1_grouped0, g1_raw0, 1)
+        quantise_g1(g1_grouped0, 0)
+
+        regroup_d1_chunk(raws[1], D1_CHUNKS[1])
+        raws[4] = load_d1(D1_CHUNKS[4])
+        g1_raw1 = load_g1(1)
+
+        for group in range(EARLY_C0_GROUPS):
+            quantise_d1(group, 0)
+            if T_GROUP * (group + 1) <= PSUM_BANKS:
+                for t in range(T_GROUP * group, T_GROUP * (group + 1)):
+                    first_core_pass(0, t, 0)
+
+        regroup_d1_chunk(raws[2], D1_CHUNKS[2])
+        g2_raw = raw_pool.tile([P, 64, P], BF16, tag="raw", name="g2_raw")
+        nc.sync.dma_start(out=g2_raw[:], in_=g2.rearrange("s (jh jl) a o -> (s jh) jl (a o)", jh=2))
+        nc.sync.dma_start(
+            out=x_rows[:], in_=x_l.rearrange("b (r j) -> (b r) j", j=P).rearrange("(q p) j -> p q j", p=P)
+        )
+        nc.sync.dma_start(
+            out=mv_rows[:], in_=mv.rearrange("b (r j) -> (b r) j", j=P).rearrange("(q p) j -> p q j", p=P)
+        )
+        nc.sync.dma_start(out=bias_rows[:], in_=bias.rearrange("(h p j) -> p h j", p=P, j=P))
+        regroup_d1_chunk(raws[3], D1_CHUNKS[3])
+
+        regroup_d1(nc.vector.tensor_copy, raws[4], D1_CHUNKS[4], 0)
+        for group in range(N_GROUPS):
+            if group + 1 < N_GROUPS:
+                regroup_d1(nc.vector.tensor_copy, raws[4], D1_CHUNKS[4], group + 1)
+            if group >= EARLY_C0_GROUPS:
+                quantise_d1(group, 0)
+            quantise_d1(group, 1)
+
+        g1_grouped1 = new_g1_grouped(1)
+        for t in range(N_T):
+            if t % T_BLOCK == 0:
+                d2_blocks[t // T_BLOCK] = big_pool.tile(
+                    [P, N_SG, T_BLOCK, 2 * M_HALF, PACK], BF16, tag="big", name="d2_block", align_bytes=64
+                )
+            if t >= PSUM_BANKS:
+                first_core_pass(0, t, 0)
+            first_core_pass(0, t, 1)
+            vector_turn = (t - VECTOR_HELPS_FROM) // 2 if (t >= VECTOR_HELPS_FROM and t % 2 == VECTOR_HELPS_FROM % 2) else -1
+            round_d2(nc.vector.tensor_copy if vector_turn >= 0 else nc.scalar.copy, 0, t)
+            if vector_turn in (0, 1):
+                regroup_g1(g1_grouped1, g1_raw1, vector_turn)
+            if vector_turn == 2:
+                quantise_g1(g1_grouped1, 1)
+
+        nc.vector.tensor_tensor(out=base[:], in0=x_rows[:], in1=mv_rows[:], op=ADD)
         for b in range(2):
-            nc.vector.tensor_tensor(out=base[:, 2 * b : 2 * b + 2, :], in0=base[:, 2 * b : 2 * b + 2, :], in1=bt[:], op=ADD)
+            nc.vector.tensor_tensor(
+                out=base[:, 2 * b : 2 * b + 2, :], in0=base[:, 2 * b : 2 * b + 2, :], in1=bias_rows[:], op=ADD
+            )
 
-        g2in = big16.tile([P, 16, 2, 64, 4], BF16, tag="big16", name="g2in", align_bytes=64)
-        codes = {}
-        for t in range(24):
-            new_acc(t)
-            pass1(1, t, 0)
-            pass1(1, t, 1)
-            evac(nc.vector.tensor_copy if t % 8 == 5 else nc.scalar.copy, 1, t)
-            if t % 8 == 7:
-                codes[t // 8] = new_codes()
-                quant_d2(t // 8, codes[t // 8][0], codes[t // 8][1], 0, 8)
-                quant_d2(t // 8, codes[t // 8][0], codes[t // 8][1], 8, 8)
-            if t % 3 == 0 and t < 12:
-                bunch = t // 3
-                tps = []
-                for half in range(2):
-                    tp = psum.tile([P, 8, 128], BF16, tag="bank", name="tp")
-                    for g in range(8):
-                        nc.tensor.transpose(tp[:, g, :], g2raw[:, 16 * bunch + 8 * half + g, :], ident[:])
-                    tps.append(tp)
-                for half in range(2):
-                    l0 = 16 * bunch + 8 * half
-                    cp = nc.vector.tensor_copy if half == 0 else nc.scalar.copy
-                    for jh in range(2):
-                        cp(
-                            out=g2in[:, :, jh, l0 : l0 + 8, :],
-                            in_=tps[half][:].rearrange("p g (sg j h) -> p h sg g j", j=4, h=2)[:, jh],
-                        )
-            if t == 9:
-                for h in range(2):
-                    nc.vector.quantize_mx(
-                        out=g2c[:, 8 * h : 8 * h + 8, :].rearrange("p sg w -> p (sg w)").bitcast(FP8X4),
-                        scales=g2s[:, 8 * h : 8 * h + 8, :].rearrange("p sg w -> p (sg w)"),
-                        in_=g2in[:, 8 * h : 8 * h + 8].rearrange("p sg h l j -> p (sg h l j)"),
-                    )
-            if t in (19, 23):
-                second_core((t - 19) // 4, codes[(t - 19) // 4][0], codes[(t - 19) // 4][1])
+        g2_grouped = big_pool.tile([P, N_SG, 2, 64, PACK], BF16, tag="big", name="g2_grouped", align_bytes=64)
+        flipped = []
+        for bank in range(PSUM_BANKS):
+            flipped.append(psum.tile([P, 8, P], BF16, tag="bank", name="flipped"))
+            for i in range(8):
+                nc.tensor.transpose(flipped[bank][:, i, :], g2_raw[:, 8 * bank + i, :], identity[:])
+        for bank in range(PSUM_BANKS):
+            copy = nc.vector.tensor_copy if bank % 2 == 0 else nc.scalar.copy
+            for jh in range(2):
+                copy(
+                    out=g2_grouped[:, :, jh, 8 * bank : 8 * (bank + 1), :],
+                    in_=flipped[bank][:].rearrange("p jl (sg si jh) -> p jh sg jl si", si=PACK, jh=2)[:, jh],
+                )
+        for sg in range(0, N_SG, 8):
+            nc.vector.quantize_mx(
+                out=g2_words[:, sg : sg + 8, :].rearrange("p sg w -> p (sg w)").bitcast(FP8X4),
+                scales=g2_scales[:, sg : sg + 8, :].rearrange("p sg w -> p (sg w)"),
+                in_=g2_grouped[:, sg : sg + 8].rearrange("p sg jh jl si -> p (sg jh jl si)"),
+            )
 
-        for t in range(24, 32):
-            new_acc(t, 256)
-            pass1(1, t, 0, 0, 256)
-            pass1(1, t, 1, 0, 256)
-            evac(nc.scalar.copy, 1, t, 0, 8)
-            if t == 27:
-                second_core(2, codes[2][0], codes[2][1])
-        cod3, sca3 = new_codes()
-        quant_d2(3, cod3, sca3, 0, 8)
-        for t in range(24, 32):
-            new_acc(t, 256)
-            pass1(1, t, 0, 256, 256)
-            pass1(1, t, 1, 256, 256)
-            evac(nc.vector.tensor_copy if t % 2 == 0 else nc.scalar.copy, 1, t, 8, 8)
-        term3 = psum.tile([P, 128], F32, tag="bank", name="term")
-        for sg in range(8):
-            pass2(term3, cod3, sca3, sg)
-        quant_d2(3, cod3, sca3, 8, 4)
-        quant_d2(3, cod3, sca3, 12, 4)
-        for sg in range(8, 16):
-            pass2(term3, cod3, sca3, sg)
-        finish(3, term3)
+        for t in range(N_T):
+            first_core_pass(1, t, 0)
+            first_core_pass(1, t, 1)
+            round_d2(nc.vector.tensor_copy if t % T_BLOCK == VECTOR_HELPS_AT else nc.scalar.copy, 1, t)
+            if t % T_BLOCK == T_BLOCK - 1:
+                quantise_block(t // T_BLOCK)
+            if t >= SECOND_CORE_FIRST_STEP and (t - SECOND_CORE_FIRST_STEP) % SECOND_CORE_STEP == 0:
+                second_core((t - SECOND_CORE_FIRST_STEP) // SECOND_CORE_STEP)

@@ -1,12 +1,12 @@
 from contextlib import ExitStack
 
 import concourse.mybir as mybir
-from concourse.masks import make_identity
 
 FLOPS = 2 * 1024 * 4096 * 1024 + 2 * 8192 * 512 * 128
 
 BF16 = mybir.dt.bfloat16
 F32 = mybir.dt.float32
+I32 = mybir.dt.int32
 U32 = mybir.dt.uint32
 U8 = mybir.dt.uint8
 FP8X4 = mybir.dt.float8_e4m3fn_x4
@@ -16,259 +16,295 @@ SUBTRACT = mybir.AluOpType.subtract
 P = 128
 PACK = 4
 N_T = 32
-N_SG = 16
-M_HALF = 8
-T_GROUP = 4
-N_GROUPS = N_T // T_GROUP
-T_BLOCK = 8
-PSUM_BANKS = 8
-SG_PER_QUANT = 4
-
-D1_CHUNKS = ((0, 0, 64, 2), (0, 64, 64, 4), (1, 0, 64, 4), (1, 64, 32, 6), (1, 96, 32, 8))
-RAW_SLOTS = 3
-
-EARLY_C0_GROUPS = 4
-VECTOR_HELPS_FROM = 17
-VECTOR_HELPS_AT = 5
-SECOND_CORE_FIRST_STEP = 19
-SECOND_CORE_STEP = 4
+N_CHUNKS = 8
+CHUNK = 512
+AG = 4
+G2_AG = 8
+N_MP = 8
+Q_M = 4
+N_Q = 4
+HALF = 64
 
 
 def tile_ttsolver_pa_kernel(tc, d1, g1, g2, x_l, mv, bias, out):
     nc = tc.nc
     with ExitStack() as ctx:
-        raw_pool = ctx.enter_context(tc.tile_pool(name="raw", bufs=RAW_SLOTS))
-        big_pool = ctx.enter_context(tc.tile_pool(name="big", bufs=5))
+        raw_pool = ctx.enter_context(tc.tile_pool(name="raw", bufs=6))
         g1_pool = ctx.enter_context(tc.tile_pool(name="g1", bufs=2))
         keep = ctx.enter_context(tc.tile_pool(name="keep", bufs=1))
-        block_pool = ctx.enter_context(tc.tile_pool(name="block", bufs=2))
-        psum = ctx.enter_context(tc.psum_pool(name="psum", bufs=PSUM_BANKS))
+        d1_pool = ctx.enter_context(tc.tile_pool(name="d1", bufs=2))
+        d1w_pool = ctx.enter_context(tc.tile_pool(name="d1w", bufs=2))
+        g2_pool = ctx.enter_context(tc.tile_pool(name="g2", bufs=2))
+        d2_pool = ctx.enter_context(tc.tile_pool(name="d2", bufs=4))
+        d2w_pool = ctx.enter_context(tc.tile_pool(name="d2w", bufs=8))
+        term_pool = ctx.enter_context(tc.psum_pool(name="terms", bufs=1))
+        psum = ctx.enter_context(tc.psum_pool(name="psum", bufs=6))
         ctx.enter_context(tc.manual_schedule())
 
-        d1_words = keep.tile([P, N_GROUPS, 2, T_GROUP * P], U32, align_bytes=64)
-        d1_scales = keep.tile([P, N_GROUPS, 2, T_GROUP * P], U8, align_bytes=64)
-        g1_words = keep.tile([P, 2, 2, 512], U32, align_bytes=64)
-        g1_scales = keep.tile([P, 2, 2, 512], U8, align_bytes=64)
-        g2_words = keep.tile([P, N_SG, P], U32, align_bytes=64)
-        g2_scales = keep.tile([P, N_SG, P], U8, align_bytes=64)
-        identity = keep.tile([P, P], BF16)
-        x_rows = keep.tile([P, 4, P], BF16)
-        mv_rows = keep.tile([P, 4, P], BF16)
-        bias_rows = keep.tile([P, 2, P], BF16)
-        base = keep.tile([P, 4, P], F32)
-
-        make_identity(nc, identity[:])
+        g1_words = keep.tile([P, N_Q, 2, 2, P], U32, align_bytes=64)
+        g1_scales = keep.tile([P, N_Q, 2, 2, P], U8, align_bytes=64)
+        g2_words = keep.tile([P, 32, 2, P], U32, align_bytes=64)
+        g2_scales = keep.tile([P, 32, 2, P], U8, align_bytes=64)
+        x_rows = keep.tile([P, 2, 256], BF16)
+        mv_rows = keep.tile([P, 2, 256], BF16)
+        bias_rows = keep.tile([P, 2, 256], BF16)
+        base = keep.tile([P, 2, 256], F32)
+        term_rows = [keep.tile([P, 256], F32, tag="result%d" % h, name="result%d" % h) for h in range(2)]
+        warm = keep.tile([P, 8], BF16)
+        terms = [term_pool.tile([P, 256], F32, tag="term%d" % h, name="term%d" % h) for h in range(2)]
 
         d1_rows = d1.rearrange("r (n a) t -> (r n) (a t)", n=16)
-        out_rows = out.rearrange("b (r j) -> (b r) j", j=P)
+
+        d1_raw = {}
+
+        def load_d1(i):
+            d1_raw[i] = raw_pool.tile([P, 2, PACK, CHUNK], BF16, tag="raw", name="d1_raw", align_bytes=64)
+            for c in range(2):
+                nc.sync.dma_start(
+                    out=d1_raw[i][:, c],
+                    in_=d1_rows[512 * c : 512 * (c + 1), i * CHUNK : (i + 1) * CHUNK].rearrange(
+                        "(p ni) w -> p ni w", ni=PACK
+                    ),
+                )
+
+        g1_raw = {}
 
         def load_g1(half):
-            raw = g1_pool.tile([P, 2, M_HALF, PACK * 64], BF16, tag="g1", name="g1_raw%d" % half, align_bytes=64)
+            raw = raw_pool.tile([P, 2, 2 * Q_M, PACK * HALF], BF16, tag="raw", name="g1_raw", align_bytes=64)
             for c in range(2):
                 for nh in range(4):
                     nc.sync.dma_start(
-                        out=raw[nh:P:4, c, :, :],
+                        out=raw[nh:P:4, c],
                         in_=g1[
-                            32 * c : 32 * c + 32, M_HALF * half : M_HALF * (half + 1), PACK * nh : PACK * (nh + 1), :
+                            32 * c : 32 * (c + 1), 8 * half : 8 * (half + 1), PACK * nh : PACK * (nh + 1), :
                         ].rearrange("r m n s -> r m (n s)"),
                     )
-            return raw
+            for q in range(2):
+                g1_raw[2 * half + q] = raw[:, :, Q_M * q : Q_M * (q + 1)]
 
-        def new_g1_grouped(half):
-            return g1_pool.tile(
-                [P, 2, N_SG, M_HALF, PACK, PACK], BF16, tag="g1", name="g1_grouped%d" % half, align_bytes=64
-            )
+        g2_raw = keep.tile([P, HALF, P], BF16, name="g2_raw", align_bytes=64)
 
-        def regroup_g1(grouped, raw, c):
-            nc.vector.tensor_copy(
-                out=grouped[:, c].rearrange("p sg m si ni -> p m sg ni si"),
-                in_=raw[:, c].rearrange("p m (ni sg si) -> p m sg ni si", ni=PACK, si=PACK),
-            )
+        def load_g2():
+            for jh in range(2):
+                nc.sync.dma_start(
+                    out=g2_raw[HALF * jh : HALF * (jh + 1)],
+                    in_=g2[:, HALF * jh : HALF * (jh + 1)].rearrange("s j a o -> s j (a o)"),
+                )
 
-        def quantise_g1(grouped, half):
+        g1_grouped = {}
+
+        def regroup_g1(copy, q):
+            grouped = g1_pool.tile([P, 2, Q_M, HALF, PACK], BF16, tag="g1", name="g1_grouped", align_bytes=64)
+            for c in range(2):
+                copy(
+                    out=grouped[:, c].rearrange("p m (sg si) ni -> p m sg ni si", si=4),
+                    in_=g1_raw[q][:, c].rearrange("p m (ni sg si) -> p m sg ni si", ni=PACK, si=4),
+                )
+            g1_grouped[q] = grouped
+
+        def quantise_g1(q):
             nc.vector.quantize_mx(
-                out=g1_words[:, half].rearrange("p c w -> p (c w)").bitcast(FP8X4),
-                scales=g1_scales[:, half].rearrange("p c w -> p (c w)"),
-                in_=grouped[:].rearrange("p c sg m si ni -> p (c sg m si ni)"),
+                out=g1_words[:, q].rearrange("p c m w -> p (c m w)").bitcast(FP8X4),
+                scales=g1_scales[:, q].rearrange("p c m w -> p (c m w)"),
+                in_=g1_grouped[q][:].rearrange("p c m s ni -> p (c m s ni)"),
             )
 
-        def load_d1(chunk):
-            c, a0, n_a = chunk[0], chunk[1], chunk[2]
-            raw = raw_pool.tile([P, PACK, n_a * N_T], BF16, tag="raw", name="d1_raw")
-            nc.sync.dma_start(
-                out=raw[:],
-                in_=d1_rows[512 * c : 512 * (c + 1), a0 * N_T : (a0 + n_a) * N_T].rearrange(
-                    "(p ni) w -> p ni w", ni=PACK
-                ),
-            )
-            return raw
+        d1_grouped = {}
+        d1_codes = {}
 
-        d1_grouped = [
-            big_pool.tile([P, 2, 2, T_GROUP, P, PACK], BF16, tag="big", name="d1_grouped%d" % i, align_bytes=64)
-            for i in range(N_GROUPS // 2)
-        ]
-
-        def regroup_d1(copy, raw, chunk, group):
-            c, a0, n_a = chunk[0], chunk[1], chunk[2]
+        def regroup_d1(copy, i, c):
+            if c == 0:
+                d1_grouped[i] = d1_pool.tile([P, 2, CHUNK, PACK], BF16, tag="d1", name="d1_grouped", align_bytes=64)
             copy(
-                out=d1_grouped[group // 2][:, group % 2, c, :, a0 : a0 + n_a, :].rearrange("p t a ni -> p a ni t"),
-                in_=raw[:].rearrange("p ni (a t) -> p a ni t", t=N_T)[:, :, :, T_GROUP * group : T_GROUP * (group + 1)],
+                out=d1_grouped[i][:, c].rearrange("p (wg wi) ni -> p wg ni wi", wi=4),
+                in_=d1_raw[i][:, c].rearrange("p ni (wg wi) -> p wg ni wi", wi=4),
             )
 
-        def regroup_d1_chunk(raw, chunk):
-            for group in range(N_GROUPS):
-                regroup_d1(nc.vector.tensor_copy if group < chunk[3] else nc.scalar.copy, raw, chunk, group)
-
-        def quantise_d1(group, c):
+        def quantise_d1(i):
+            words = d1w_pool.tile([P, 2, CHUNK], U32, tag="words", name="d1_words", align_bytes=64)
+            scales = d1w_pool.tile([P, 2, CHUNK], U8, tag="scales", name="d1_scales", align_bytes=64)
             nc.vector.quantize_mx(
-                out=d1_words[:, group, c, :].bitcast(FP8X4),
-                scales=d1_scales[:, group, c, :],
-                in_=d1_grouped[group // 2][:, group % 2, c].rearrange("p t a ni -> p (t a ni)"),
+                out=words[:].rearrange("p c w -> p (c w)").bitcast(FP8X4),
+                scales=scales[:].rearrange("p c w -> p (c w)"),
+                in_=d1_grouped[i][:].rearrange("p c w ni -> p (c w ni)"),
             )
+            d1_codes[i] = (words, scales)
+
+        g2_grouped = {}
+        g2_codes = {}
+
+        def regroup_g2(copy, i):
+            g2_grouped[i] = g2_pool.tile([P, G2_AG, HALF, PACK], BF16, tag="g2", name="g2_grouped", align_bytes=64)
+            words = g2_grouped[i][:].rearrange("p ag j ai -> p (ag j ai)").bitcast(F32).rearrange("p (ag j u) -> p ag j u", j=HALF, u=2)
+            raw = g2_raw[:].rearrange("p j a -> p (j a)").bitcast(F32).rearrange("p (j ag u) -> p ag j u", j=HALF, u=2)
+            copy(out=words, in_=raw[:, G2_AG * i : G2_AG * (i + 1)])
+
+        def quantise_g2(i):
+            words = g2_pool.tile([P, G2_AG, HALF], U32, tag="words", name="g2_tmp_words", align_bytes=64)
+            scales = g2_pool.tile([P, G2_AG, HALF], U8, tag="scales", name="g2_tmp_scales", align_bytes=64)
+            nc.vector.quantize_mx(
+                out=words[:].rearrange("p ag j -> p (ag j)").bitcast(FP8X4),
+                scales=scales[:].rearrange("p ag j -> p (ag j)"),
+                in_=g2_grouped[i][:].rearrange("p ag j ai -> p (ag j ai)"),
+            )
+            g2_codes[i] = (words, scales)
+
+        def place_g2(i):
+            words, scales = g2_codes[i]
+            for par in range(2):
+                rows = slice(HALF * par, HALF * (par + 1))
+                for jh in range(2):
+                    source = slice(HALF * jh, HALF * (jh + 1))
+                    nc.sync.dma_start(
+                        out=g2_words[rows, G2_AG * i : G2_AG * (i + 1), par, source].bitcast(I32),
+                        in_=words[source].bitcast(I32),
+                    )
+                    for quad in range(2):
+                        live = 32 * quad
+                        nc.sync.dma_start(
+                            out=g2_scales[
+                                HALF * par + live : HALF * par + live + 4, G2_AG * i : G2_AG * (i + 1), par, source
+                            ].bitcast(I32),
+                            in_=scales[HALF * jh + live : HALF * jh + live + 4].bitcast(I32),
+                        )
 
         sums = {}
-        d2_blocks = {}
+        d2_tiles = {}
+        d2_codes = {}
 
-        def first_core_pass(half, t, c):
-            if c == 0:
-                sums[t] = psum.tile([P, 512], F32, tag="bank", name="sums")
-            columns = slice(P * (t % T_GROUP), P * (t % T_GROUP + 1))
-            nc.tensor.matmul_mx(
-                out=sums[t][:],
-                lhsT=d1_words[:, t // T_GROUP, c, columns].bitcast(FP8X4),
-                lhsT_scale=d1_scales[:, t // T_GROUP, c, columns],
-                rhs=g1_words[:, half, c, :].bitcast(FP8X4),
-                rhs_scale=g1_scales[:, half, c, :],
-                start=(c == 0),
-                stop=(c == 1),
-            )
-
-        def round_d2(copy, half, t):
-            copy(
-                out=d2_blocks[t // T_BLOCK][:, :, t % T_BLOCK, M_HALF * half : M_HALF * (half + 1), :],
-                in_=sums[t][:].rearrange("p (sg m si) -> p sg m si", m=M_HALF, si=PACK),
-            )
-
-        block_codes = {}
-
-        def quantise_block(q):
-            words = block_pool.tile([P, N_SG, P], U32, tag="words", name="d2_words", align_bytes=64)
-            scales = block_pool.tile([P, N_SG, P], U8, tag="scales", name="d2_scales", align_bytes=64)
-            block_codes[q] = (words, scales)
-            for sg in range(0, N_SG, SG_PER_QUANT):
-                part = slice(sg, sg + SG_PER_QUANT)
-                nc.vector.quantize_mx(
-                    out=words[:, part, :].rearrange("p sg w -> p (sg w)").bitcast(FP8X4),
-                    scales=scales[:, part, :].rearrange("p sg w -> p (sg w)"),
-                    in_=d2_blocks[q][:, part].rearrange("p sg t m si -> p (sg t m si)"),
-                )
-
-        def second_core(q):
-            words, scales = block_codes[q]
-            term = psum.tile([P, P], F32, tag="bank", name="term")
-            for sg in range(N_SG):
+        def first_core(i, mp):
+            words, scales = d1_codes[i]
+            sums[mp] = psum.tile([P, CHUNK], F32, tag="bank", name="sums")
+            for c in range(2):
                 nc.tensor.matmul_mx(
-                    out=term[:],
-                    lhsT=words[:, sg, :].bitcast(FP8X4),
-                    lhsT_scale=scales[:, sg, :],
-                    rhs=g2_words[:, sg, :].bitcast(FP8X4),
-                    rhs_scale=g2_scales[:, sg, :],
-                    start=(sg == 0),
-                    stop=(sg == N_SG - 1),
+                    out=sums[mp][:],
+                    lhsT=g1_words[:, mp // 2, c, mp % 2, :].bitcast(FP8X4),
+                    lhsT_scale=g1_scales[:, mp // 2, c, mp % 2, :],
+                    rhs=words[:, c, :].bitcast(FP8X4),
+                    rhs_scale=scales[:, c, :],
+                    start=(c == 0),
+                    stop=(c == 1),
                 )
-            result = block_pool.tile([P, P], F32, tag="result", name="result")
-            nc.vector.tensor_tensor(out=result[:], in0=base[:, q, :], in1=term[:], op=SUBTRACT)
-            nc.sync.dma_start(out=out_rows[P * q : P * (q + 1), :], in_=result[:])
 
-        raws = {0: load_d1(D1_CHUNKS[0])}
-        g1_raw0 = load_g1(0)
-        raws[1] = load_d1(D1_CHUNKS[1])
-        raws[2] = load_d1(D1_CHUNKS[2])
-
-        regroup_d1_chunk(raws[0], D1_CHUNKS[0])
-        raws[3] = load_d1(D1_CHUNKS[3])
-        g1_grouped0 = new_g1_grouped(0)
-        regroup_g1(g1_grouped0, g1_raw0, 0)
-        regroup_g1(g1_grouped0, g1_raw0, 1)
-        quantise_g1(g1_grouped0, 0)
-
-        regroup_d1_chunk(raws[1], D1_CHUNKS[1])
-        raws[4] = load_d1(D1_CHUNKS[4])
-        g1_raw1 = load_g1(1)
-
-        for group in range(EARLY_C0_GROUPS):
-            quantise_d1(group, 0)
-            if T_GROUP * (group + 1) <= PSUM_BANKS:
-                for t in range(T_GROUP * group, T_GROUP * (group + 1)):
-                    first_core_pass(0, t, 0)
-
-        regroup_d1_chunk(raws[2], D1_CHUNKS[2])
-        g2_raw = raw_pool.tile([P, 64, P], BF16, tag="raw", name="g2_raw")
-        nc.sync.dma_start(out=g2_raw[:], in_=g2.rearrange("s (jh jl) a o -> (s jh) jl (a o)", jh=2))
-        nc.sync.dma_start(
-            out=x_rows[:], in_=x_l.rearrange("b (r j) -> (b r) j", j=P).rearrange("(q p) j -> p q j", p=P)
-        )
-        nc.sync.dma_start(
-            out=mv_rows[:], in_=mv.rearrange("b (r j) -> (b r) j", j=P).rearrange("(q p) j -> p q j", p=P)
-        )
-        nc.sync.dma_start(out=bias_rows[:], in_=bias.rearrange("(h p j) -> p h j", p=P, j=P))
-        regroup_d1_chunk(raws[3], D1_CHUNKS[3])
-
-        regroup_d1(nc.vector.tensor_copy, raws[4], D1_CHUNKS[4], 0)
-        for group in range(N_GROUPS):
-            if group + 1 < N_GROUPS:
-                regroup_d1(nc.vector.tensor_copy, raws[4], D1_CHUNKS[4], group + 1)
-            if group >= EARLY_C0_GROUPS:
-                quantise_d1(group, 0)
-            quantise_d1(group, 1)
-
-        g1_grouped1 = new_g1_grouped(1)
-        for t in range(N_T):
-            if t % T_BLOCK == 0:
-                d2_blocks[t // T_BLOCK] = big_pool.tile(
-                    [P, N_SG, T_BLOCK, 2 * M_HALF, PACK], BF16, tag="big", name="d2_block", align_bytes=64
-                )
-            if t >= PSUM_BANKS:
-                first_core_pass(0, t, 0)
-            first_core_pass(0, t, 1)
-            vector_turn = (t - VECTOR_HELPS_FROM) // 2 if (t >= VECTOR_HELPS_FROM and t % 2 == VECTOR_HELPS_FROM % 2) else -1
-            round_d2(nc.vector.tensor_copy if vector_turn >= 0 else nc.scalar.copy, 0, t)
-            if vector_turn in (0, 1):
-                regroup_g1(g1_grouped1, g1_raw1, vector_turn)
-            if vector_turn == 2:
-                quantise_g1(g1_grouped1, 1)
-
-        nc.vector.tensor_tensor(out=base[:], in0=x_rows[:], in1=mv_rows[:], op=ADD)
-        for b in range(2):
-            nc.vector.tensor_tensor(
-                out=base[:, 2 * b : 2 * b + 2, :], in0=base[:, 2 * b : 2 * b + 2, :], in1=bias_rows[:], op=ADD
+        def round_d2(copy, i, mp):
+            h = mp // 4
+            if mp % 4 == 0:
+                d2_tiles[(i, h)] = d2_pool.tile([P, AG, 4, N_T, PACK], BF16, tag="d2", name="d2", align_bytes=64)
+            copy(
+                out=d2_tiles[(i, h)][:, :, mp % 4],
+                in_=sums[mp][:].rearrange("p (ag ai t) -> p ag t ai", ai=PACK, t=N_T),
             )
 
-        g2_grouped = big_pool.tile([P, N_SG, 2, 64, PACK], BF16, tag="big", name="g2_grouped", align_bytes=64)
-        flipped = []
-        for bank in range(PSUM_BANKS):
-            flipped.append(psum.tile([P, 8, P], BF16, tag="bank", name="flipped"))
-            for i in range(8):
-                nc.tensor.transpose(flipped[bank][:, i, :], g2_raw[:, 8 * bank + i, :], identity[:])
-        for bank in range(PSUM_BANKS):
-            copy = nc.vector.tensor_copy if bank % 2 == 0 else nc.scalar.copy
-            for jh in range(2):
-                copy(
-                    out=g2_grouped[:, :, jh, 8 * bank : 8 * (bank + 1), :],
-                    in_=flipped[bank][:].rearrange("p jl (sg si jh) -> p jh sg jl si", si=PACK, jh=2)[:, jh],
-                )
-        for sg in range(0, N_SG, 8):
+        def quantise_d2(i, h):
+            words = d2w_pool.tile([P, AG, P], U32, tag="words", name="d2_words", align_bytes=64)
+            scales = d2w_pool.tile([P, AG, P], U8, tag="scales", name="d2_scales", align_bytes=64)
             nc.vector.quantize_mx(
-                out=g2_words[:, sg : sg + 8, :].rearrange("p sg w -> p (sg w)").bitcast(FP8X4),
-                scales=g2_scales[:, sg : sg + 8, :].rearrange("p sg w -> p (sg w)"),
-                in_=g2_grouped[:, sg : sg + 8].rearrange("p sg jh jl si -> p (sg jh jl si)"),
+                out=words[:].rearrange("p ag w -> p (ag w)").bitcast(FP8X4),
+                scales=scales[:].rearrange("p ag w -> p (ag w)"),
+                in_=d2_tiles[(i, h)][:].rearrange("p ag mp t ai -> p (ag mp t ai)"),
             )
+            d2_codes[(i, h)] = (words, scales)
 
-        for t in range(N_T):
-            first_core_pass(1, t, 0)
-            first_core_pass(1, t, 1)
-            round_d2(nc.vector.tensor_copy if t % T_BLOCK == VECTOR_HELPS_AT else nc.scalar.copy, 1, t)
-            if t % T_BLOCK == T_BLOCK - 1:
-                quantise_block(t // T_BLOCK)
-            if t >= SECOND_CORE_FIRST_STEP and (t - SECOND_CORE_FIRST_STEP) % SECOND_CORE_STEP == 0:
-                second_core((t - SECOND_CORE_FIRST_STEP) // SECOND_CORE_STEP)
+        def second_core(i, h):
+            words, scales = d2_codes[(i, h)]
+            for ag in range(AG):
+                nc.tensor.matmul_mx(
+                    out=terms[h][:],
+                    lhsT=words[:, ag, :].bitcast(FP8X4),
+                    lhsT_scale=scales[:, ag, :],
+                    rhs=g2_words[:, AG * i + ag].rearrange("p par j -> p (par j)").bitcast(FP8X4),
+                    rhs_scale=g2_scales[:, AG * i + ag].rearrange("p par j -> p (par j)"),
+                    start=(i == 0 and ag == 0),
+                    stop=(i == N_CHUNKS - 1 and ag == AG - 1),
+                )
+
+        def out_view(ap):
+            return ap.rearrange("b (m0 h q f) -> (b m0) h q f", h=2, q=4, f=256)
+
+        def finish(h):
+            result = term_rows[h]
+            nc.vector.tensor_tensor(out=result[:], in0=base[:, h, :], in1=terms[h][:], op=SUBTRACT)
+            for q in range(4):
+                queue = nc.sync if q % 2 == 0 else nc.scalar
+                queue.dma_start(out=out_view(out)[:, h, q, :], in_=result[N_T * q : N_T * (q + 1), :])
+
+        load_g1(0)
+        load_d1(0)
+        load_g1(1)
+        for i in range(1, 4):
+            load_d1(i)
+        load_g2()
+        for i in range(4, N_CHUNKS):
+            load_d1(i)
+        for q in range(4):
+            rows = slice(N_T * q, N_T * (q + 1))
+            nc.sync.dma_start(out=x_rows[rows], in_=out_view(x_l)[:, :, q, :])
+            nc.sync.dma_start(out=mv_rows[rows], in_=out_view(mv)[:, :, q, :])
+            for b in range(2):
+                nc.sync.dma_start(
+                    out=bias_rows[N_T * q + 16 * b : N_T * q + 16 * (b + 1)],
+                    in_=bias.rearrange("(m0 h q f) -> m0 h q f", h=2, q=4, f=256)[:, :, q, :],
+                )
+
+        V = nc.vector.tensor_copy
+        S = nc.scalar.copy
+        nc.vector.memset(warm[:], 0.0)
+        S(out=warm[:, 4:8], in_=warm[:, 0:4])
+        nc.vector.memset(g2_words[HALF:P, 0:16, 0, :], 0)
+        nc.gpsimd.memset(g2_words[0:HALF, :, 1, :], 0)
+        nc.gpsimd.memset(g2_words[HALF:P, 16:32, 0, :], 0)
+        nc.gpsimd.memset(g2_scales[:].rearrange("p ag par j -> p (ag par j)").bitcast(I32), 0)
+
+        regroup_g1(S, 0)
+        regroup_g1(V, 1)
+        regroup_d1(V, 0, 0)
+        quantise_g1(0)
+        regroup_d1(V, 0, 1)
+        quantise_g1(1)
+        quantise_d1(0)
+        regroup_g1(S, 2)
+        regroup_g1(V, 3)
+        regroup_d1(V, 1, 0)
+        quantise_g1(2)
+        quantise_g1(3)
+
+        pending = []
+
+        def issue(count):
+            for n in range(min(count, len(pending))):
+                second_core(*pending.pop(0))
+
+        G2_STEPS = {(2, 2): 0, (3, 2): 1, (3, 5): 2, (4, 2): 3}
+        for i in range(N_CHUNKS):
+            for mp in range(N_MP):
+                first_core(i, mp)
+                if i == 0 and mp == 1:
+                    regroup_d1(S, 1, 1)
+                round_d2(V if i == 7 and mp == 5 else S, i, mp)
+                if mp == (3 if i == 0 else 0) and i + 1 < N_CHUNKS:
+                    quantise_d1(i + 1)
+                if mp == 1 and i > 0:
+                    quantise_d2(i - 1, 1)
+                    pending.append((i - 1, 1))
+                if mp == 2 and i + 2 < N_CHUNKS:
+                    regroup_d1(V, i + 2, 0)
+                if mp == 4 and i + 2 < N_CHUNKS:
+                    regroup_d1(V, i + 2, 1)
+                if mp == 5:
+                    quantise_d2(i, 0)
+                    pending.append((i, 0))
+                if (i, mp) in G2_STEPS:
+                    regroup_g2(S, G2_STEPS[(i, mp)])
+                if (i, mp - 2) in G2_STEPS:
+                    quantise_g2(G2_STEPS[(i, mp - 2)])
+                    place_g2(G2_STEPS[(i, mp - 2)])
+                if mp in (2, 6) and i > 3:
+                    issue(2)
+                if i == 6 and mp == 7:
+                    nc.vector.tensor_tensor(out=base[:], in0=x_rows[:], in1=mv_rows[:], op=ADD)
+                    nc.vector.tensor_tensor(out=base[:], in0=base[:], in1=bias_rows[:], op=ADD)
+        issue(len(pending))
+        finish(0)
+        quantise_d2(N_CHUNKS - 1, 1)
+        second_core(N_CHUNKS - 1, 1)
+        finish(1)

@@ -29,7 +29,9 @@ HALF = 64
 def tile_ttsolver_pa_kernel(tc, d1, g1, g2, x_l, mv, bias, out):
     nc = tc.nc
     with ExitStack() as ctx:
-        raw_pool = ctx.enter_context(tc.tile_pool(name="raw", bufs=6))
+        raw_pool = ctx.enter_context(tc.tile_pool(name="raw", bufs=4))
+        pair_pool = ctx.enter_context(tc.tile_pool(name="pair", bufs=2))
+        spread_pool = ctx.enter_context(tc.tile_pool(name="spread", bufs=N_CHUNKS // 2))
         g1_pool = ctx.enter_context(tc.tile_pool(name="g1", bufs=2))
         keep = ctx.enter_context(tc.tile_pool(name="keep", bufs=1))
         d1_pool = ctx.enter_context(tc.tile_pool(name="d1", bufs=2))
@@ -45,6 +47,7 @@ def tile_ttsolver_pa_kernel(tc, d1, g1, g2, x_l, mv, bias, out):
         g1_scales = keep.tile([P, N_Q, 2, 2, P], U8, align_bytes=64)
         g2_words = keep.tile([P, 32, 2, P], U32, align_bytes=64)
         g2_scales = keep.tile([P, 32, 2, P], U8, align_bytes=64)
+        spread_scales = keep.tile([P, 32, HALF], U8, align_bytes=64)
         x_rows = keep.tile([P, 2, 256], BF16)
         mv_rows = keep.tile([P, 2, 256], BF16)
         bias_rows = keep.tile([P, 2, 256], BF16)
@@ -57,15 +60,18 @@ def tile_ttsolver_pa_kernel(tc, d1, g1, g2, x_l, mv, bias, out):
 
         d1_raw = {}
 
-        def load_d1(i):
-            d1_raw[i] = raw_pool.tile([P, 2, PACK, CHUNK], BF16, tag="raw", name="d1_raw", align_bytes=64)
+        def load_d1(first, count):
+            pool = raw_pool if count == 1 else pair_pool
+            raw = pool.tile([P, 2, PACK, count * CHUNK], BF16, tag="raw", name="d1_raw", align_bytes=64)
             for c in range(2):
                 nc.sync.dma_start(
-                    out=d1_raw[i][:, c],
-                    in_=d1_rows[512 * c : 512 * (c + 1), i * CHUNK : (i + 1) * CHUNK].rearrange(
+                    out=raw[:, c],
+                    in_=d1_rows[512 * c : 512 * (c + 1), first * CHUNK : (first + count) * CHUNK].rearrange(
                         "(p ni) w -> p ni w", ni=PACK
                     ),
                 )
+            for i in range(count):
+                d1_raw[first + i] = raw[:, :, :, i * CHUNK : (i + 1) * CHUNK]
 
         g1_raw = {}
 
@@ -135,22 +141,25 @@ def tile_ttsolver_pa_kernel(tc, d1, g1, g2, x_l, mv, bias, out):
 
         def regroup_g2(copy, i):
             g2_grouped[i] = g2_pool.tile([P, G2_AG, HALF, PACK], BF16, tag="g2", name="g2_grouped", align_bytes=64)
-            words = g2_grouped[i][:].rearrange("p ag j ai -> p (ag j ai)").bitcast(F32).rearrange("p (ag j u) -> p ag j u", j=HALF, u=2)
-            raw = g2_raw[:].rearrange("p j a -> p (j a)").bitcast(F32).rearrange("p (j ag u) -> p ag j u", j=HALF, u=2)
-            copy(out=words, in_=raw[:, G2_AG * i : G2_AG * (i + 1)])
+            words = g2_grouped[i][:].rearrange("p ag j ai -> p (ag j ai)").bitcast(F32)
+            raw = g2_raw[:].rearrange("p j a -> p (j a)").bitcast(F32)
+            copy(
+                out=words.rearrange("p (ag jg ji u) -> p jg ag ji u", ag=G2_AG, ji=4, u=2),
+                in_=raw.rearrange("p (jg ji ag u) -> p jg ag ji u", jg=HALF // 4, ji=4, u=2)[:, :, G2_AG * i : G2_AG * (i + 1)],
+            )
 
         def quantise_g2(i):
-            words = g2_pool.tile([P, G2_AG, HALF], U32, tag="words", name="g2_tmp_words", align_bytes=64)
-            scales = g2_pool.tile([P, G2_AG, HALF], U8, tag="scales", name="g2_tmp_scales", align_bytes=64)
+            words = spread_pool.tile([P, G2_AG, HALF], U32, tag="words", name="g2_tmp_words", align_bytes=64)
+            scales = spread_scales[:, G2_AG * i : G2_AG * (i + 1)]
             nc.vector.quantize_mx(
                 out=words[:].rearrange("p ag j -> p (ag j)").bitcast(FP8X4),
-                scales=scales[:].rearrange("p ag j -> p (ag j)"),
+                scales=scales.rearrange("p ag j -> p (ag j)"),
                 in_=g2_grouped[i][:].rearrange("p ag j ai -> p (ag j ai)"),
             )
-            g2_codes[i] = (words, scales)
+            g2_codes[i] = words
 
         def place_g2(i):
-            words, scales = g2_codes[i]
+            words = g2_codes[i]
             for par in range(2):
                 rows = slice(HALF * par, HALF * (par + 1))
                 for jh in range(2):
@@ -159,13 +168,17 @@ def tile_ttsolver_pa_kernel(tc, d1, g1, g2, x_l, mv, bias, out):
                         out=g2_words[rows, G2_AG * i : G2_AG * (i + 1), par, source].bitcast(I32),
                         in_=words[source].bitcast(I32),
                     )
-                    for quad in range(2):
-                        live = 32 * quad
+
+        def place_g2_scales(first, count):
+            groups = slice(G2_AG * first, G2_AG * (first + count))
+            for par in range(2):
+                for jh in range(2):
+                    for live in (0, 32):
                         nc.sync.dma_start(
                             out=g2_scales[
-                                HALF * par + live : HALF * par + live + 4, G2_AG * i : G2_AG * (i + 1), par, source
+                                HALF * par + live : HALF * par + live + 4, groups, par, HALF * jh : HALF * (jh + 1)
                             ].bitcast(I32),
-                            in_=scales[HALF * jh + live : HALF * jh + live + 4].bitcast(I32),
+                            in_=spread_scales[HALF * jh + live : HALF * jh + live + 4, groups].bitcast(I32),
                         )
 
         sums = {}
@@ -229,13 +242,13 @@ def tile_ttsolver_pa_kernel(tc, d1, g1, g2, x_l, mv, bias, out):
                 queue.dma_start(out=out_view(out)[:, h, q, :], in_=result[N_T * q : N_T * (q + 1), :])
 
         load_g1(0)
-        load_d1(0)
+        load_d1(0, 1)
         load_g1(1)
-        for i in range(1, 4):
-            load_d1(i)
+        load_d1(1, 1)
+        load_d1(2, 2)
         load_g2()
-        for i in range(4, N_CHUNKS):
-            load_d1(i)
+        load_d1(4, 2)
+        load_d1(6, 2)
         for q in range(4):
             rows = slice(N_T * q, N_T * (q + 1))
             nc.sync.dma_start(out=x_rows[rows], in_=out_view(x_l)[:, :, q, :])
@@ -250,10 +263,9 @@ def tile_ttsolver_pa_kernel(tc, d1, g1, g2, x_l, mv, bias, out):
         S = nc.scalar.copy
         nc.vector.memset(warm[:], 0.0)
         S(out=warm[:, 4:8], in_=warm[:, 0:4])
-        nc.vector.memset(g2_words[HALF:P, 0:16, 0, :], 0)
         nc.gpsimd.memset(g2_words[0:HALF, :, 1, :], 0)
-        nc.gpsimd.memset(g2_words[HALF:P, 16:32, 0, :], 0)
-        nc.gpsimd.memset(g2_scales[:].rearrange("p ag par j -> p (ag par j)").bitcast(I32), 0)
+        nc.vector.memset(g2_words[HALF:P, :, 0, :], 0)
+        nc.vector.memset(g2_scales[:].rearrange("p ag par j -> p (ag par j)").bitcast(I32), 0)
 
         regroup_g1(S, 0)
         regroup_g1(V, 1)
@@ -274,7 +286,7 @@ def tile_ttsolver_pa_kernel(tc, d1, g1, g2, x_l, mv, bias, out):
             for n in range(min(count, len(pending))):
                 second_core(*pending.pop(0))
 
-        G2_STEPS = {(2, 2): 0, (3, 2): 1, (3, 5): 2, (4, 2): 3}
+        G2_STEPS = {(2, 1): 0, (2, 5): 1, (3, 1): 2, (3, 5): 3}
         for i in range(N_CHUNKS):
             for mp in range(N_MP):
                 first_core(i, mp)
@@ -298,6 +310,8 @@ def tile_ttsolver_pa_kernel(tc, d1, g1, g2, x_l, mv, bias, out):
                 if (i, mp - 2) in G2_STEPS:
                     quantise_g2(G2_STEPS[(i, mp - 2)])
                     place_g2(G2_STEPS[(i, mp - 2)])
+                    if mp == 7:
+                        place_g2_scales(2 * (i - 2), 2)
                 if mp in (2, 6) and i > 3:
                     issue(2)
                 if i == 6 and mp == 7:

@@ -38,7 +38,7 @@ def tile_ttsolver_pa_kernel(tc, d1, g1, g2, x_l, mv, bias, out):
         d1w_pool = ctx.enter_context(tc.tile_pool(name="d1w", bufs=2))
         g2_pool = ctx.enter_context(tc.tile_pool(name="g2", bufs=2))
         d2_pool = ctx.enter_context(tc.tile_pool(name="d2", bufs=4))
-        d2w_pool = ctx.enter_context(tc.tile_pool(name="d2w", bufs=8))
+        d2w_pool = ctx.enter_context(tc.tile_pool(name="d2w", bufs=10))
         term_pool = ctx.enter_context(tc.psum_pool(name="terms", bufs=1))
         psum = ctx.enter_context(tc.psum_pool(name="psum", bufs=6))
         ctx.enter_context(tc.manual_schedule())
@@ -60,11 +60,11 @@ def tile_ttsolver_pa_kernel(tc, d1, g1, g2, x_l, mv, bias, out):
 
         d1_raw = {}
 
-        def load_d1(first, count):
+        def load_d1(queue, first, count):
             pool = raw_pool if count == 1 else pair_pool
             raw = pool.tile([P, 2, PACK, count * CHUNK], BF16, tag="raw", name="d1_raw", align_bytes=64)
             for c in range(2):
-                nc.sync.dma_start(
+                queue.dma_start(
                     out=raw[:, c],
                     in_=d1_rows[512 * c : 512 * (c + 1), first * CHUNK : (first + count) * CHUNK].rearrange(
                         "(p ni) w -> p ni w", ni=PACK
@@ -91,8 +91,8 @@ def tile_ttsolver_pa_kernel(tc, d1, g1, g2, x_l, mv, bias, out):
         g2_raw = keep.tile([P, HALF, P], BF16, name="g2_raw", align_bytes=64)
 
         def load_g2():
-            for jh in range(2):
-                nc.sync.dma_start(
+            for jh, queue in enumerate((nc.sync, nc.scalar)):
+                queue.dma_start(
                     out=g2_raw[HALF * jh : HALF * (jh + 1)],
                     in_=g2[:, HALF * jh : HALF * (jh + 1)].rearrange("s j a o -> s j (a o)"),
                 )
@@ -242,13 +242,12 @@ def tile_ttsolver_pa_kernel(tc, d1, g1, g2, x_l, mv, bias, out):
                 queue.dma_start(out=out_view(out)[:, h, q, :], in_=result[N_T * q : N_T * (q + 1), :])
 
         load_g1(0)
-        load_d1(0, 1)
+        load_d1(nc.sync, 0, 1)
         load_g1(1)
-        load_d1(1, 1)
-        load_d1(2, 2)
+        load_d1(nc.sync, 1, 1)
+        load_d1(nc.sync, 2, 2)
         load_g2()
-        load_d1(4, 2)
-        load_d1(6, 2)
+        load_d1(nc.sync, 4, 2)
         for q in range(4):
             rows = slice(N_T * q, N_T * (q + 1))
             nc.sync.dma_start(out=x_rows[rows], in_=out_view(x_l)[:, :, q, :])
@@ -263,9 +262,10 @@ def tile_ttsolver_pa_kernel(tc, d1, g1, g2, x_l, mv, bias, out):
         S = nc.scalar.copy
         nc.vector.memset(warm[:], 0.0)
         S(out=warm[:, 4:8], in_=warm[:, 0:4])
-        nc.gpsimd.memset(g2_words[0:HALF, :, 1, :], 0)
+        nc.gpsimd.memset(g2_scales[:].rearrange("p ag par j -> p (ag par j)").bitcast(I32), 0)
+        nc.gpsimd.memset(g2_words[0:HALF, 0:16, 1, :], 0)
         nc.vector.memset(g2_words[HALF:P, :, 0, :], 0)
-        nc.vector.memset(g2_scales[:].rearrange("p ag par j -> p (ag par j)").bitcast(I32), 0)
+        nc.vector.memset(g2_words[0:HALF, 16:32, 1, :], 0)
 
         regroup_g1(S, 0)
         regroup_g1(V, 1)
@@ -286,7 +286,7 @@ def tile_ttsolver_pa_kernel(tc, d1, g1, g2, x_l, mv, bias, out):
             for n in range(min(count, len(pending))):
                 second_core(*pending.pop(0))
 
-        G2_STEPS = {(2, 1): 0, (2, 5): 1, (3, 1): 2, (3, 5): 3}
+        G2_STEPS = {(2, 3): 0, (2, 6): 1, (3, 2): 2, (3, 5): 3}
         for i in range(N_CHUNKS):
             for mp in range(N_MP):
                 first_core(i, mp)
@@ -307,12 +307,14 @@ def tile_ttsolver_pa_kernel(tc, d1, g1, g2, x_l, mv, bias, out):
                     pending.append((i, 0))
                 if (i, mp) in G2_STEPS:
                     regroup_g2(S, G2_STEPS[(i, mp)])
-                if (i, mp - 2) in G2_STEPS:
-                    quantise_g2(G2_STEPS[(i, mp - 2)])
-                    place_g2(G2_STEPS[(i, mp - 2)])
-                    if mp == 7:
+                if (i, mp - 1) in G2_STEPS:
+                    quantise_g2(G2_STEPS[(i, mp - 1)])
+                    place_g2(G2_STEPS[(i, mp - 1)])
+                    if G2_STEPS[(i, mp - 1)] % 2 == 1:
                         place_g2_scales(2 * (i - 2), 2)
-                if mp in (2, 6) and i > 3:
+                if i == 2 and mp == 0:
+                    load_d1(nc.scalar, 6, 2)
+                if mp in (1, 4, 7) and i > 4:
                     issue(2)
                 if i == 6 and mp == 7:
                     nc.vector.tensor_tensor(out=base[:], in0=x_rows[:], in1=mv_rows[:], op=ADD)

@@ -103,8 +103,8 @@ def tile_ttsolver_pa_kernel(tc, d1, g1, g2, x_l, mv, bias, out):
             grouped = g1_pool.tile([P, 2, Q_M, HALF, PACK], BF16, tag="g1", name="g1_grouped", align_bytes=64)
             for c in range(2):
                 copy(
-                    out=grouped[:, c].rearrange("p m (sg si) ni -> p m sg ni si", si=4),
-                    in_=g1_raw[q][:, c].rearrange("p m (ni sg si) -> p m sg ni si", ni=PACK, si=4),
+                    out=grouped[:, c],
+                    in_=g1_raw[q][:, c].rearrange("p m (ni s) -> p m s ni", ni=PACK),
                 )
             g1_grouped[q] = grouped
 
@@ -122,8 +122,8 @@ def tile_ttsolver_pa_kernel(tc, d1, g1, g2, x_l, mv, bias, out):
             if c == 0:
                 d1_grouped[i] = d1_pool.tile([P, 2, CHUNK, PACK], BF16, tag="d1", name="d1_grouped", align_bytes=64)
             copy(
-                out=d1_grouped[i][:, c].rearrange("p (wg wi) ni -> p wg ni wi", wi=4),
-                in_=d1_raw[i][:, c].rearrange("p ni (wg wi) -> p wg ni wi", wi=4),
+                out=d1_grouped[i][:, c],
+                in_=d1_raw[i][:, c].rearrange("p ni w -> p w ni"),
             )
 
         def quantise_d1(i):

@@ -204,8 +204,8 @@ def tile_ttsolver_pa_kernel(tc, d1, g1, g2, x_l, mv, bias, out):
             if mp % 4 == 0:
                 d2_tiles[(i, h)] = d2_pool.tile([P, AG, 4, N_T, PACK], BF16, tag="d2", name="d2", align_bytes=64)
             copy(
-                out=d2_tiles[(i, h)][:, :, mp % 4],
-                in_=sums[mp][:].rearrange("p (ag ai t) -> p ag t ai", ai=PACK, t=N_T),
+                out=d2_tiles[(i, h)][:, :, mp % 4].rearrange("p ag (tg ti) ai -> p ag tg ai ti", ti=4),
+                in_=sums[mp][:].rearrange("p (ag ai tg ti) -> p ag tg ai ti", ag=AG, ai=PACK, ti=4),
             )
 
         def quantise_d2(i, h):

@@ -37,8 +37,8 @@ def tile_ttsolver_pa_kernel(tc, d1, g1, g2, x_l, mv, bias, out):
         d1_pool = ctx.enter_context(tc.tile_pool(name="d1", bufs=2))
         d1w_pool = ctx.enter_context(tc.tile_pool(name="d1w", bufs=2))
         g2_pool = ctx.enter_context(tc.tile_pool(name="g2", bufs=2))
-        d2_pool = ctx.enter_context(tc.tile_pool(name="d2", bufs=4))
-        d2w_pool = ctx.enter_context(tc.tile_pool(name="d2w", bufs=10))
+        d2_pool = ctx.enter_context(tc.tile_pool(name="d2", bufs=3))
+        d2w_pool = ctx.enter_context(tc.tile_pool(name="d2w", bufs=14))
         term_pool = ctx.enter_context(tc.psum_pool(name="terms", bufs=1))
         psum = ctx.enter_context(tc.psum_pool(name="psum", bufs=6))
         ctx.enter_context(tc.manual_schedule())
@@ -314,7 +314,7 @@ def tile_ttsolver_pa_kernel(tc, d1, g1, g2, x_l, mv, bias, out):
                         place_g2_scales(2 * (i - 2), 2)
                 if i == 2 and mp == 0:
                     load_d1(nc.scalar, 6, 2)
-                if mp in (1, 4, 7) and i > 4:
+                if i == N_CHUNKS - 1:
                     issue(2)
                 if i == 6 and mp == 7:
                     nc.vector.tensor_tensor(out=base[:], in0=x_rows[:], in1=mv_rows[:], op=ADD)

@@ -31,14 +31,13 @@ def tile_ttsolver_pa_kernel(tc, d1, g1, g2, x_l, mv, bias, out):
     with ExitStack() as ctx:
         raw_pool = ctx.enter_context(tc.tile_pool(name="raw", bufs=4))
         pair_pool = ctx.enter_context(tc.tile_pool(name="pair", bufs=2))
-        spread_pool = ctx.enter_context(tc.tile_pool(name="spread", bufs=N_CHUNKS // 2))
         g1_pool = ctx.enter_context(tc.tile_pool(name="g1", bufs=2))
         keep = ctx.enter_context(tc.tile_pool(name="keep", bufs=1))
         d1_pool = ctx.enter_context(tc.tile_pool(name="d1", bufs=2))
         d1w_pool = ctx.enter_context(tc.tile_pool(name="d1w", bufs=2))
-        g2_pool = ctx.enter_context(tc.tile_pool(name="g2", bufs=2))
+        g2_pool = ctx.enter_context(tc.tile_pool(name="g2", bufs=1))
         d2_pool = ctx.enter_context(tc.tile_pool(name="d2", bufs=3))
-        d2w_pool = ctx.enter_context(tc.tile_pool(name="d2w", bufs=14))
+        d2w_pool = ctx.enter_context(tc.tile_pool(name="d2w", bufs=16))
         term_pool = ctx.enter_context(tc.psum_pool(name="terms", bufs=1))
         psum = ctx.enter_context(tc.psum_pool(name="psum", bufs=6))
         ctx.enter_context(tc.manual_schedule())
@@ -47,12 +46,12 @@ def tile_ttsolver_pa_kernel(tc, d1, g1, g2, x_l, mv, bias, out):
         g1_scales = keep.tile([P, N_Q, 2, 2, P], U8, align_bytes=64)
         g2_words = keep.tile([P, 32, 2, P], U32, align_bytes=64)
         g2_scales = keep.tile([P, 32, 2, P], U8, align_bytes=64)
-        spread_scales = keep.tile([P, 32, HALF], U8, align_bytes=64)
+        half_words = keep.tile([P, 32, HALF], U32, align_bytes=64)
+        half_scales = keep.tile([P, 32, HALF], U8, align_bytes=64)
         x_rows = keep.tile([P, 2, 256], BF16)
         mv_rows = keep.tile([P, 2, 256], BF16)
         bias_rows = keep.tile([P, 2, 256], BF16)
         base = keep.tile([P, 2, 256], F32)
-        term_rows = [keep.tile([P, 256], F32, tag="result%d" % h, name="result%d" % h) for h in range(2)]
         warm = keep.tile([P, 8], BF16)
         terms = [term_pool.tile([P, 256], F32, tag="term%d" % h, name="term%d" % h) for h in range(2)]
 
@@ -60,11 +59,11 @@ def tile_ttsolver_pa_kernel(tc, d1, g1, g2, x_l, mv, bias, out):
 
         d1_raw = {}
 
-        def load_d1(queue, first, count):
+        def load_d1(first, count):
             pool = raw_pool if count == 1 else pair_pool
             raw = pool.tile([P, 2, PACK, count * CHUNK], BF16, tag="raw", name="d1_raw", align_bytes=64)
             for c in range(2):
-                queue.dma_start(
+                nc.sync.dma_start(
                     out=raw[:, c],
                     in_=d1_rows[512 * c : 512 * (c + 1), first * CHUNK : (first + count) * CHUNK].rearrange(
                         "(p ni) w -> p ni w", ni=PACK
@@ -90,12 +89,11 @@ def tile_ttsolver_pa_kernel(tc, d1, g1, g2, x_l, mv, bias, out):
 
         g2_raw = keep.tile([P, HALF, P], BF16, name="g2_raw", align_bytes=64)
 
-        def load_g2():
-            for jh, queue in enumerate((nc.sync, nc.scalar)):
-                queue.dma_start(
-                    out=g2_raw[HALF * jh : HALF * (jh + 1)],
-                    in_=g2[:, HALF * jh : HALF * (jh + 1)].rearrange("s j a o -> s j (a o)"),
-                )
+        def load_g2(queue, jh):
+            queue.dma_start(
+                out=g2_raw[HALF * jh : HALF * (jh + 1)],
+                in_=g2[:, HALF * jh : HALF * (jh + 1)].rearrange("s j a o -> s j (a o)"),
+            )
 
         g1_grouped = {}
 
@@ -137,7 +135,6 @@ def tile_ttsolver_pa_kernel(tc, d1, g1, g2, x_l, mv, bias, out):
             d1_codes[i] = (words, scales)
 
         g2_grouped = {}
-        g2_codes = {}
 
         def regroup_g2(copy, i):
             g2_grouped[i] = g2_pool.tile([P, G2_AG, HALF, PACK], BF16, tag="g2", name="g2_grouped", align_bytes=64)
@@ -149,36 +146,29 @@ def tile_ttsolver_pa_kernel(tc, d1, g1, g2, x_l, mv, bias, out):
             )
 
         def quantise_g2(i):
-            words = spread_pool.tile([P, G2_AG, HALF], U32, tag="words", name="g2_tmp_words", align_bytes=64)
-            scales = spread_scales[:, G2_AG * i : G2_AG * (i + 1)]
+            groups = slice(G2_AG * i, G2_AG * (i + 1))
             nc.vector.quantize_mx(
-                out=words[:].rearrange("p ag j -> p (ag j)").bitcast(FP8X4),
-                scales=scales.rearrange("p ag j -> p (ag j)"),
+                out=half_words[:, groups].rearrange("p ag j -> p (ag j)").bitcast(FP8X4),
+                scales=half_scales[:, groups].rearrange("p ag j -> p (ag j)"),
                 in_=g2_grouped[i][:].rearrange("p ag j ai -> p (ag j ai)"),
             )
-            g2_codes[i] = words
 
-        def place_g2(i):
-            words = g2_codes[i]
+        def spread_g2():
             for par in range(2):
-                rows = slice(HALF * par, HALF * (par + 1))
                 for jh in range(2):
-                    source = slice(HALF * jh, HALF * (jh + 1))
+                    columns = slice(HALF * jh, HALF * (jh + 1))
                     nc.sync.dma_start(
-                        out=g2_words[rows, G2_AG * i : G2_AG * (i + 1), par, source].bitcast(I32),
-                        in_=words[source].bitcast(I32),
+                        out=g2_words[HALF * par : HALF * (par + 1), :, par, columns].bitcast(I32),
+                        in_=half_words[columns].bitcast(I32),
                     )
-
-        def place_g2_scales(first, count):
-            groups = slice(G2_AG * first, G2_AG * (first + count))
             for par in range(2):
                 for jh in range(2):
                     for live in (0, 32):
                         nc.sync.dma_start(
                             out=g2_scales[
-                                HALF * par + live : HALF * par + live + 4, groups, par, HALF * jh : HALF * (jh + 1)
+                                HALF * par + live : HALF * par + live + 4, :, par, HALF * jh : HALF * (jh + 1)
                             ].bitcast(I32),
-                            in_=spread_scales[HALF * jh + live : HALF * jh + live + 4, groups].bitcast(I32),
+                            in_=half_scales[HALF * jh + live : HALF * jh + live + 4].bitcast(I32),
                         )
 
         sums = {}
@@ -235,29 +225,16 @@ def tile_ttsolver_pa_kernel(tc, d1, g1, g2, x_l, mv, bias, out):
             return ap.rearrange("b (m0 h q f) -> (b m0) h q f", h=2, q=4, f=256)
 
         def finish(h):
-            result = term_rows[h]
-            nc.vector.tensor_tensor(out=result[:], in0=base[:, h, :], in1=terms[h][:], op=SUBTRACT)
+            result = base[:, h, :]
+            nc.vector.tensor_tensor(out=result, in0=result, in1=terms[h][:], op=SUBTRACT)
             for q in range(4):
                 queue = nc.sync if q % 2 == 0 else nc.scalar
-                queue.dma_start(out=out_view(out)[:, h, q, :], in_=result[N_T * q : N_T * (q + 1), :])
+                queue.dma_start(out=out_view(out)[:, h, q, :], in_=base[N_T * q : N_T * (q + 1), h, :])
 
+        load_d1(0, 1)
         load_g1(0)
-        load_d1(nc.sync, 0, 1)
         load_g1(1)
-        load_d1(nc.sync, 1, 1)
-        load_d1(nc.sync, 2, 2)
-        load_g2()
-        load_d1(nc.sync, 4, 2)
-        for q in range(4):
-            rows = slice(N_T * q, N_T * (q + 1))
-            nc.sync.dma_start(out=x_rows[rows], in_=out_view(x_l)[:, :, q, :])
-            nc.sync.dma_start(out=mv_rows[rows], in_=out_view(mv)[:, :, q, :])
-            for b in range(2):
-                nc.sync.dma_start(
-                    out=bias_rows[N_T * q + 16 * b : N_T * q + 16 * (b + 1)],
-                    in_=bias.rearrange("(m0 h q f) -> m0 h q f", h=2, q=4, f=256)[:, :, q, :],
-                )
-
+        load_d1(1, 1)
         V = nc.vector.tensor_copy
         S = nc.scalar.copy
         nc.vector.memset(warm[:], 0.0)
@@ -267,24 +244,33 @@ def tile_ttsolver_pa_kernel(tc, d1, g1, g2, x_l, mv, bias, out):
         nc.vector.memset(g2_words[HALF:P, :, 0, :], 0)
         nc.vector.memset(g2_words[0:HALF, 16:32, 1, :], 0)
 
+        regroup_d1(V, 0, 0)
+        regroup_d1(V, 0, 1)
         regroup_g1(S, 0)
         regroup_g1(V, 1)
-        regroup_d1(V, 0, 0)
+        load_d1(2, 1)
         quantise_g1(0)
-        regroup_d1(V, 0, 1)
-        quantise_g1(1)
+        load_d1(3, 1)
         quantise_d1(0)
         regroup_g1(S, 2)
+        quantise_g1(1)
+        load_g2(nc.sync, 0)
+        load_g2(nc.scalar, 1)
+        load_d1(4, 2)
+        load_d1(6, 2)
+        for q in range(4):
+            rows = slice(N_T * q, N_T * (q + 1))
+            nc.sync.dma_start(out=x_rows[rows], in_=out_view(x_l)[:, :, q, :])
+            nc.sync.dma_start(out=mv_rows[rows], in_=out_view(mv)[:, :, q, :])
+            for b in range(2):
+                nc.sync.dma_start(
+                    out=bias_rows[N_T * q + 16 * b : N_T * q + 16 * (b + 1)],
+                    in_=bias.rearrange("(m0 h q f) -> m0 h q f", h=2, q=4, f=256)[:, :, q, :],
+                )
         regroup_g1(V, 3)
         regroup_d1(V, 1, 0)
         quantise_g1(2)
         quantise_g1(3)
-
-        pending = []
-
-        def issue(count):
-            for n in range(min(count, len(pending))):
-                second_core(*pending.pop(0))
 
         G2_STEPS = {(2, 3): 0, (2, 6): 1, (3, 2): 2, (3, 5): 3}
         for i in range(N_CHUNKS):
@@ -292,35 +278,28 @@ def tile_ttsolver_pa_kernel(tc, d1, g1, g2, x_l, mv, bias, out):
                 first_core(i, mp)
                 if i == 0 and mp == 1:
                     regroup_d1(S, 1, 1)
-                round_d2(V if i == 7 and mp == 5 else S, i, mp)
+                round_d2(V if i == 7 and mp == 6 else S, i, mp)
                 if mp == (3 if i == 0 else 0) and i + 1 < N_CHUNKS:
                     quantise_d1(i + 1)
                 if mp == 1 and i > 0:
                     quantise_d2(i - 1, 1)
-                    pending.append((i - 1, 1))
                 if mp == 2 and i + 2 < N_CHUNKS:
                     regroup_d1(V, i + 2, 0)
                 if mp == 4 and i + 2 < N_CHUNKS:
                     regroup_d1(V, i + 2, 1)
                 if mp == 5:
                     quantise_d2(i, 0)
-                    pending.append((i, 0))
                 if (i, mp) in G2_STEPS:
                     regroup_g2(S, G2_STEPS[(i, mp)])
                 if (i, mp - 1) in G2_STEPS:
                     quantise_g2(G2_STEPS[(i, mp - 1)])
-                    place_g2(G2_STEPS[(i, mp - 1)])
-                    if G2_STEPS[(i, mp - 1)] % 2 == 1:
-                        place_g2_scales(2 * (i - 2), 2)
-                if i == 2 and mp == 0:
-                    load_d1(nc.scalar, 6, 2)
-                if i == N_CHUNKS - 1:
-                    issue(2)
+                if i == 3 and mp == 7:
+                    spread_g2()
                 if i == 6 and mp == 7:
                     nc.vector.tensor_tensor(out=base[:], in0=x_rows[:], in1=mv_rows[:], op=ADD)
                     nc.vector.tensor_tensor(out=base[:], in0=base[:], in1=bias_rows[:], op=ADD)
-        issue(len(pending))
-        finish(0)
         quantise_d2(N_CHUNKS - 1, 1)
-        second_core(N_CHUNKS - 1, 1)
-        finish(1)
+        for h in range(2):
+            for i in range(N_CHUNKS):
+                second_core(i, h)
+            finish(h)

@@ -153,23 +153,24 @@ def tile_ttsolver_pa_kernel(tc, d1, g1, g2, x_l, mv, bias, out):
                 in_=g2_grouped[i][:].rearrange("p ag j ai -> p (ag j ai)"),
             )
 
-        def spread_g2():
+        def cross_g2(groups):
             for par in range(2):
-                for jh in range(2):
-                    columns = slice(HALF * jh, HALF * (jh + 1))
+                jh = 1 - par
+                columns = slice(HALF * jh, HALF * (jh + 1))
+                nc.sync.dma_start(
+                    out=g2_words[HALF * par : HALF * (par + 1), groups, par, columns].bitcast(I32),
+                    in_=half_words[columns, groups].bitcast(I32),
+                )
+                for live in (0, 32):
                     nc.sync.dma_start(
-                        out=g2_words[HALF * par : HALF * (par + 1), :, par, columns].bitcast(I32),
-                        in_=half_words[columns].bitcast(I32),
+                        out=g2_scales[HALF * par + live : HALF * par + live + 4, groups, par, columns].bitcast(I32),
+                        in_=half_scales[HALF * jh + live : HALF * jh + live + 4, groups].bitcast(I32),
                     )
-            for par in range(2):
-                for jh in range(2):
-                    for live in (0, 32):
-                        nc.sync.dma_start(
-                            out=g2_scales[
-                                HALF * par + live : HALF * par + live + 4, :, par, HALF * jh : HALF * (jh + 1)
-                            ].bitcast(I32),
-                            in_=half_scales[HALF * jh + live : HALF * jh + live + 4].bitcast(I32),
-                        )
+
+        def keep_g2(par):
+            rows = slice(HALF * par, HALF * (par + 1))
+            nc.vector.tensor_copy(out=g2_words[rows, :, par, rows].bitcast(I32), in_=half_words[rows].bitcast(I32))
+            nc.vector.tensor_copy(out=g2_scales[rows, :, par, rows].bitcast(I32), in_=half_scales[rows].bitcast(I32))
 
         sums = {}
         d2_tiles = {}
@@ -241,6 +242,7 @@ def tile_ttsolver_pa_kernel(tc, d1, g1, g2, x_l, mv, bias, out):
         S(out=warm[:, 4:8], in_=warm[:, 0:4])
         nc.gpsimd.memset(g2_scales[:].rearrange("p ag par j -> p (ag par j)").bitcast(I32), 0)
         nc.gpsimd.memset(g2_words[0:HALF, 0:16, 1, :], 0)
+        nc.vector.memset(half_scales[:].rearrange("p ag j -> p (ag j)").bitcast(I32), 0)
         nc.vector.memset(g2_words[HALF:P, :, 0, :], 0)
         nc.vector.memset(g2_words[0:HALF, 16:32, 1, :], 0)
 
@@ -293,8 +295,10 @@ def tile_ttsolver_pa_kernel(tc, d1, g1, g2, x_l, mv, bias, out):
                     regroup_g2(S, G2_STEPS[(i, mp)])
                 if (i, mp - 1) in G2_STEPS:
                     quantise_g2(G2_STEPS[(i, mp - 1)])
-                if i == 3 and mp == 7:
-                    spread_g2()
+                if i == 3 and mp in (0, 7):
+                    cross_g2(slice(16 * (mp // 7), 16 * (mp // 7 + 1)))
+                if i == 6 and mp in (2, 4):
+                    keep_g2(mp // 2 - 1)
                 if i == 6 and mp == 7:
                     nc.vector.tensor_tensor(out=base[:], in0=x_rows[:], in1=mv_rows[:], op=ADD)
                     nc.vector.tensor_tensor(out=base[:], in0=base[:], in1=bias_rows[:], op=ADD)

@@ -195,8 +195,8 @@ def tile_ttsolver_pa_kernel(tc, d1, g1, g2, x_l, mv, bias, out):
             if mp % 4 == 0:
                 d2_tiles[(i, h)] = d2_pool.tile([P, AG, 4, N_T, PACK], BF16, tag="d2", name="d2", align_bytes=64)
             copy(
-                out=d2_tiles[(i, h)][:, :, mp % 4].rearrange("p ag (tg ti) ai -> p ag tg ai ti", ti=4),
-                in_=sums[mp][:].rearrange("p (ag ai tg ti) -> p ag tg ai ti", ag=AG, ai=PACK, ti=4),
+                out=d2_tiles[(i, h)][:, :, mp % 4],
+                in_=sums[mp][:].rearrange("p (ag ai t) -> p ag t ai", ai=PACK, t=N_T),
             )
 
         def quantise_d2(i, h):

@@ -35,9 +35,8 @@ def tile_ttsolver_pa_kernel(tc, d1, g1, g2, x_l, mv, bias, out):
         keep = ctx.enter_context(tc.tile_pool(name="keep", bufs=1))
         d1_pool = ctx.enter_context(tc.tile_pool(name="d1", bufs=2))
         d1w_pool = ctx.enter_context(tc.tile_pool(name="d1w", bufs=2))
-        g2_pool = ctx.enter_context(tc.tile_pool(name="g2", bufs=1))
-        d2_pool = ctx.enter_context(tc.tile_pool(name="d2", bufs=3))
-        d2w_pool = ctx.enter_context(tc.tile_pool(name="d2w", bufs=16))
+        d2_pool = ctx.enter_context(tc.tile_pool(name="d2", bufs=2))
+        d2w_pool = ctx.enter_context(tc.tile_pool(name="d2w", bufs=8))
         term_pool = ctx.enter_context(tc.psum_pool(name="terms", bufs=1))
         psum = ctx.enter_context(tc.psum_pool(name="psum", bufs=6))
         ctx.enter_context(tc.manual_schedule())
@@ -116,13 +115,10 @@ def tile_ttsolver_pa_kernel(tc, d1, g1, g2, x_l, mv, bias, out):
         d1_grouped = {}
         d1_codes = {}
 
-        def regroup_d1(copy, i, c):
-            if c == 0:
+        def regroup_d1(copy, i, halves):
+            if i not in d1_grouped:
                 d1_grouped[i] = d1_pool.tile([P, 2, CHUNK, PACK], BF16, tag="d1", name="d1_grouped", align_bytes=64)
-            copy(
-                out=d1_grouped[i][:, c],
-                in_=d1_raw[i][:, c].rearrange("p ni w -> p w ni"),
-            )
+            copy(out=d1_grouped[i][:, halves], in_=d1_raw[i][:, halves].rearrange("p c ni w -> p c w ni"))
 
         def quantise_d1(i):
             words = d1w_pool.tile([P, 2, CHUNK], U32, tag="words", name="d1_words", align_bytes=64)
@@ -137,7 +133,7 @@ def tile_ttsolver_pa_kernel(tc, d1, g1, g2, x_l, mv, bias, out):
         g2_grouped = {}
 
         def regroup_g2(copy, i):
-            g2_grouped[i] = g2_pool.tile([P, G2_AG, HALF, PACK], BF16, tag="g2", name="g2_grouped", align_bytes=64)
+            g2_grouped[i] = g1_pool.tile([P, G2_AG, HALF, PACK], BF16, tag="g1", name="g2_grouped", align_bytes=64)
             words = g2_grouped[i][:].rearrange("p ag j ai -> p (ag j ai)").bitcast(F32)
             raw = g2_raw[:].rearrange("p j a -> p (j a)").bitcast(F32)
             copy(
@@ -167,10 +163,15 @@ def tile_ttsolver_pa_kernel(tc, d1, g1, g2, x_l, mv, bias, out):
                         in_=half_scales[HALF * jh + live : HALF * jh + live + 4, groups].bitcast(I32),
                     )
 
-        def keep_g2(par):
-            rows = slice(HALF * par, HALF * (par + 1))
-            nc.vector.tensor_copy(out=g2_words[rows, :, par, rows].bitcast(I32), in_=half_words[rows].bitcast(I32))
-            nc.vector.tensor_copy(out=g2_scales[rows, :, par, rows].bitcast(I32), in_=half_scales[rows].bitcast(I32))
+        def keep_g2(groups):
+            for par in range(2):
+                rows = slice(HALF * par, HALF * (par + 1))
+                nc.vector.tensor_copy(
+                    out=g2_words[rows, groups, par, rows].bitcast(I32), in_=half_words[rows, groups].bitcast(I32)
+                )
+                nc.vector.tensor_copy(
+                    out=g2_scales[rows, groups, par, rows].bitcast(I32), in_=half_scales[rows, groups].bitcast(I32)
+                )
 
         sums = {}
         d2_tiles = {}
@@ -191,31 +192,30 @@ def tile_ttsolver_pa_kernel(tc, d1, g1, g2, x_l, mv, bias, out):
                 )
 
         def round_d2(copy, i, mp):
-            h = mp // 4
-            if mp % 4 == 0:
-                d2_tiles[(i, h)] = d2_pool.tile([P, AG, 4, N_T, PACK], BF16, tag="d2", name="d2", align_bytes=64)
+            if mp == 0:
+                d2_tiles[i] = d2_pool.tile([P, 2, AG, 4, N_T, PACK], BF16, tag="d2", name="d2", align_bytes=64)
             copy(
-                out=d2_tiles[(i, h)][:, :, mp % 4],
+                out=d2_tiles[i][:, mp // 4, :, mp % 4],
                 in_=sums[mp][:].rearrange("p (ag ai t) -> p ag t ai", ai=PACK, t=N_T),
             )
 
-        def quantise_d2(i, h):
-            words = d2w_pool.tile([P, AG, P], U32, tag="words", name="d2_words", align_bytes=64)
-            scales = d2w_pool.tile([P, AG, P], U8, tag="scales", name="d2_scales", align_bytes=64)
+        def quantise_d2(i):
+            words = d2w_pool.tile([P, 2, AG, P], U32, tag="words", name="d2_words", align_bytes=64)
+            scales = d2w_pool.tile([P, 2, AG, P], U8, tag="scales", name="d2_scales", align_bytes=64)
             nc.vector.quantize_mx(
-                out=words[:].rearrange("p ag w -> p (ag w)").bitcast(FP8X4),
-                scales=scales[:].rearrange("p ag w -> p (ag w)"),
-                in_=d2_tiles[(i, h)][:].rearrange("p ag mp t ai -> p (ag mp t ai)"),
+                out=words[:].rearrange("p h ag w -> p (h ag w)").bitcast(FP8X4),
+                scales=scales[:].rearrange("p h ag w -> p (h ag w)"),
+                in_=d2_tiles[i][:].rearrange("p h ag mp t ai -> p (h ag mp t ai)"),
             )
-            d2_codes[(i, h)] = (words, scales)
+            d2_codes[i] = (words, scales)
 
         def second_core(i, h):
-            words, scales = d2_codes[(i, h)]
+            words, scales = d2_codes[i]
             for ag in range(AG):
                 nc.tensor.matmul_mx(
                     out=terms[h][:],
-                    lhsT=words[:, ag, :].bitcast(FP8X4),
-                    lhsT_scale=scales[:, ag, :],
+                    lhsT=words[:, h, ag, :].bitcast(FP8X4),
+                    lhsT_scale=scales[:, h, ag, :],
                     rhs=g2_words[:, AG * i + ag].rearrange("p par j -> p (par j)").bitcast(FP8X4),
                     rhs_scale=g2_scales[:, AG * i + ag].rearrange("p par j -> p (par j)"),
                     start=(i == 0 and ag == 0),
@@ -243,11 +243,11 @@ def tile_ttsolver_pa_kernel(tc, d1, g1, g2, x_l, mv, bias, out):
         nc.gpsimd.memset(g2_scales[:].rearrange("p ag par j -> p (ag par j)").bitcast(I32), 0)
         nc.gpsimd.memset(g2_words[0:HALF, 0:16, 1, :], 0)
         nc.vector.memset(half_scales[:].rearrange("p ag j -> p (ag j)").bitcast(I32), 0)
-        nc.vector.memset(g2_words[HALF:P, :, 0, :], 0)
-        nc.vector.memset(g2_words[0:HALF, 16:32, 1, :], 0)
+        nc.vector.memset(g2_words[HALF:P, :, 0, :].bitcast(I32), 0)
+        nc.vector.memset(g2_words[0:HALF, 16:32, 1, :].bitcast(I32), 0)
 
-        regroup_d1(V, 0, 0)
-        regroup_d1(V, 0, 1)
+        regroup_d1(V, 0, slice(0, 1))
+        regroup_d1(V, 0, slice(1, 2))
         regroup_g1(S, 0)
         regroup_g1(V, 1)
         load_d1(2, 1)
@@ -256,10 +256,9 @@ def tile_ttsolver_pa_kernel(tc, d1, g1, g2, x_l, mv, bias, out):
         quantise_d1(0)
         regroup_g1(S, 2)
         quantise_g1(1)
-        load_g2(nc.sync, 0)
-        load_g2(nc.scalar, 1)
         load_d1(4, 2)
         load_d1(6, 2)
+        load_g2(nc.sync, 0)
         for q in range(4):
             rows = slice(N_T * q, N_T * (q + 1))
             nc.sync.dma_start(out=x_rows[rows], in_=out_view(x_l)[:, :, q, :])
@@ -270,40 +269,38 @@ def tile_ttsolver_pa_kernel(tc, d1, g1, g2, x_l, mv, bias, out):
                     in_=bias.rearrange("(m0 h q f) -> m0 h q f", h=2, q=4, f=256)[:, :, q, :],
                 )
         regroup_g1(V, 3)
-        regroup_d1(V, 1, 0)
+        regroup_d1(V, 1, slice(0, 1))
         quantise_g1(2)
         quantise_g1(3)
 
-        G2_STEPS = {(2, 3): 0, (2, 6): 1, (3, 2): 2, (3, 5): 3}
+        G2_STEPS = {(5, 5): 0, (6, 0): 1, (6, 3): 2, (6, 4): 3}
         for i in range(N_CHUNKS):
             for mp in range(N_MP):
                 first_core(i, mp)
                 if i == 0 and mp == 1:
-                    regroup_d1(S, 1, 1)
+                    regroup_d1(S, 1, slice(1, 2))
                 round_d2(V if i == 7 and mp == 6 else S, i, mp)
-                if mp == (3 if i == 0 else 0) and i + 1 < N_CHUNKS:
+                if mp == (2 if i == 0 else 0) and i + 1 < N_CHUNKS:
                     quantise_d1(i + 1)
                 if mp == 1 and i > 0:
-                    quantise_d2(i - 1, 1)
+                    quantise_d2(i - 1)
                 if mp == 2 and i + 2 < N_CHUNKS:
-                    regroup_d1(V, i + 2, 0)
-                if mp == 4 and i + 2 < N_CHUNKS:
-                    regroup_d1(V, i + 2, 1)
-                if mp == 5:
-                    quantise_d2(i, 0)
-                if (i, mp) in G2_STEPS:
-                    regroup_g2(S, G2_STEPS[(i, mp)])
+                    regroup_d1(V, i + 2, slice(0, 2))
                 if (i, mp - 1) in G2_STEPS:
-                    quantise_g2(G2_STEPS[(i, mp - 1)])
-                if i == 3 and mp in (0, 7):
-                    cross_g2(slice(16 * (mp // 7), 16 * (mp // 7 + 1)))
-                if i == 6 and mp in (2, 4):
-                    keep_g2(mp // 2 - 1)
-                if i == 6 and mp == 7:
-                    nc.vector.tensor_tensor(out=base[:], in0=x_rows[:], in1=mv_rows[:], op=ADD)
-                    nc.vector.tensor_tensor(out=base[:], in0=base[:], in1=bias_rows[:], op=ADD)
-        quantise_d2(N_CHUNKS - 1, 1)
-        for h in range(2):
-            for i in range(N_CHUNKS):
+                    piece = G2_STEPS[(i, mp - 1)]
+                    quantise_g2(piece)
+                    cross_g2(slice(G2_AG * piece, G2_AG * (piece + 1)))
+                if (i, mp) in G2_STEPS:
+                    regroup_g2(V if G2_STEPS[(i, mp)] == 3 else S, G2_STEPS[(i, mp)])
+                if i == 4 and mp == 0:
+                    load_g2(nc.scalar, 1)
+                if i == 7 and mp in (2, 5):
+                    keep_g2(slice(16 * (mp // 5), 16 * (mp // 5 + 1)))
+        quantise_d2(N_CHUNKS - 1)
+        nc.vector.tensor_tensor(out=base[:], in0=x_rows[:], in1=mv_rows[:], op=ADD)
+        nc.vector.tensor_tensor(out=base[:], in0=base[:], in1=bias_rows[:], op=ADD)
+        for i in range(N_CHUNKS):
+            for h in range(2):
                 second_core(i, h)
+        for h in range(2):
             finish(h)

from contextlib import ExitStack

import concourse.mybir as mybir

FLOPS = 2 * 1024 * 4096 * 1024 + 2 * 8192 * 512 * 128

BF16 = mybir.dt.bfloat16
F32 = mybir.dt.float32
I32 = mybir.dt.int32
U32 = mybir.dt.uint32
U8 = mybir.dt.uint8
FP8X4 = mybir.dt.float8_e4m3fn_x4
ADD = mybir.AluOpType.add
SUBTRACT = mybir.AluOpType.subtract

P = 128
PACK = 4
N_T = 32
N_CHUNKS = 8
CHUNK = 512
AG = 4
G2_AG = 8
N_MP = 8
Q_M = 4
N_Q = 4
HALF = 64


def tile_ttsolver_pa_kernel(tc, d1, g1, g2, x_l, mv, bias, out):
    nc = tc.nc
    with ExitStack() as ctx:
        raw_pool = ctx.enter_context(tc.tile_pool(name="raw", bufs=4))
        pair_pool = ctx.enter_context(tc.tile_pool(name="pair", bufs=2))
        g1_pool = ctx.enter_context(tc.tile_pool(name="g1", bufs=2))
        keep = ctx.enter_context(tc.tile_pool(name="keep", bufs=1))
        d1_pool = ctx.enter_context(tc.tile_pool(name="d1", bufs=2))
        d1w_pool = ctx.enter_context(tc.tile_pool(name="d1w", bufs=2))
        d2_pool = ctx.enter_context(tc.tile_pool(name="d2", bufs=2))
        d2w_pool = ctx.enter_context(tc.tile_pool(name="d2w", bufs=8))
        term_pool = ctx.enter_context(tc.psum_pool(name="terms", bufs=1))
        psum = ctx.enter_context(tc.psum_pool(name="psum", bufs=6))
        ctx.enter_context(tc.manual_schedule())

        g1_words = keep.tile([P, N_Q, 2, 2, P], U32, align_bytes=64)
        g1_scales = keep.tile([P, N_Q, 2, 2, P], U8, align_bytes=64)
        g2_words = keep.tile([P, 32, 2, P], U32, align_bytes=64)
        g2_scales = keep.tile([P, 32, 2, P], U8, align_bytes=64)
        half_words = keep.tile([P, 32, HALF], U32, align_bytes=64)
        half_scales = keep.tile([P, 32, HALF], U8, align_bytes=64)
        x_rows = keep.tile([P, 2, 256], BF16)
        mv_rows = keep.tile([P, 2, 256], BF16)
        bias_rows = keep.tile([P, 2, 256], BF16)
        base = keep.tile([P, 2, 256], F32)
        warm = keep.tile([P, 8], BF16)
        terms = [term_pool.tile([P, 256], F32, tag="term%d" % h, name="term%d" % h) for h in range(2)]

        d1_rows = d1.rearrange("r (n a) t -> (r n) (a t)", n=16)

        d1_raw = {}

        def load_d1(first, count):
            pool = raw_pool if count == 1 else pair_pool
            raw = pool.tile([P, 2, PACK, count * CHUNK], BF16, tag="raw", name="d1_raw", align_bytes=64)
            for c in range(2):
                nc.sync.dma_start(
                    out=raw[:, c],
                    in_=d1_rows[512 * c : 512 * (c + 1), first * CHUNK : (first + count) * CHUNK].rearrange(
                        "(p ni) w -> p ni w", ni=PACK
                    ),
                )
            for i in range(count):
                d1_raw[first + i] = raw[:, :, :, i * CHUNK : (i + 1) * CHUNK]

        g1_raw = {}

        def load_g1(half):
            raw = raw_pool.tile([P, 2, 2 * Q_M, PACK * HALF], BF16, tag="raw", name="g1_raw", align_bytes=64)
            for c in range(2):
                for nh in range(4):
                    nc.sync.dma_start(
                        out=raw[nh:P:4, c],
                        in_=g1[
                            32 * c : 32 * (c + 1), 8 * half : 8 * (half + 1), PACK * nh : PACK * (nh + 1), :
                        ].rearrange("r m n s -> r m (n s)"),
                    )
            for q in range(2):
                g1_raw[2 * half + q] = raw[:, :, Q_M * q : Q_M * (q + 1)]

        g2_raw = keep.tile([P, HALF, P], BF16, name="g2_raw", align_bytes=64)

        def load_g2(queue, jh):
            queue.dma_start(
                out=g2_raw[HALF * jh : HALF * (jh + 1)],
                in_=g2[:, HALF * jh : HALF * (jh + 1)].rearrange("s j a o -> s j (a o)"),
            )

        g1_grouped = {}

        def regroup_g1(copy, q):
            grouped = g1_pool.tile([P, 2, Q_M, HALF, PACK], BF16, tag="g1", name="g1_grouped", align_bytes=64)
            for c in range(2):
                copy(
                    out=grouped[:, c],
                    in_=g1_raw[q][:, c].rearrange("p m (ni s) -> p m s ni", ni=PACK),
                )
            g1_grouped[q] = grouped

        def quantise_g1(q):
            nc.vector.quantize_mx(
                out=g1_words[:, q].rearrange("p c m w -> p (c m w)").bitcast(FP8X4),
                scales=g1_scales[:, q].rearrange("p c m w -> p (c m w)"),
                in_=g1_grouped[q][:].rearrange("p c m s ni -> p (c m s ni)"),
            )

        d1_grouped = {}
        d1_codes = {}

        def regroup_d1(copy, i, halves):
            if i not in d1_grouped:
                d1_grouped[i] = d1_pool.tile([P, 2, CHUNK, PACK], BF16, tag="d1", name="d1_grouped", align_bytes=64)
            copy(out=d1_grouped[i][:, halves], in_=d1_raw[i][:, halves].rearrange("p c ni w -> p c w ni"))

        def quantise_d1(i):
            words = d1w_pool.tile([P, 2, CHUNK], U32, tag="words", name="d1_words", align_bytes=64)
            scales = d1w_pool.tile([P, 2, CHUNK], U8, tag="scales", name="d1_scales", align_bytes=64)
            nc.vector.quantize_mx(
                out=words[:].rearrange("p c w -> p (c w)").bitcast(FP8X4),
                scales=scales[:].rearrange("p c w -> p (c w)"),
                in_=d1_grouped[i][:].rearrange("p c w ni -> p (c w ni)"),
            )
            d1_codes[i] = (words, scales)

        g2_grouped = {}

        def regroup_g2(copy, i):
            g2_grouped[i] = g1_pool.tile([P, G2_AG, HALF, PACK], BF16, tag="g1", name="g2_grouped", align_bytes=64)
            words = g2_grouped[i][:].rearrange("p ag j ai -> p (ag j ai)").bitcast(F32)
            raw = g2_raw[:].rearrange("p j a -> p (j a)").bitcast(F32)
            copy(
                out=words.rearrange("p (ag jg ji u) -> p jg ag ji u", ag=G2_AG, ji=4, u=2),
                in_=raw.rearrange("p (jg ji ag u) -> p jg ag ji u", jg=HALF // 4, ji=4, u=2)[:, :, G2_AG * i : G2_AG * (i + 1)],
            )

        def quantise_g2(i):
            groups = slice(G2_AG * i, G2_AG * (i + 1))
            nc.vector.quantize_mx(
                out=half_words[:, groups].rearrange("p ag j -> p (ag j)").bitcast(FP8X4),
                scales=half_scales[:, groups].rearrange("p ag j -> p (ag j)"),
                in_=g2_grouped[i][:].rearrange("p ag j ai -> p (ag j ai)"),
            )

        def cross_g2(groups):
            for par in range(2):
                jh = 1 - par
                columns = slice(HALF * jh, HALF * (jh + 1))
                nc.sync.dma_start(
                    out=g2_words[HALF * par : HALF * (par + 1), groups, par, columns].bitcast(I32),
                    in_=half_words[columns, groups].bitcast(I32),
                )
                for live in (0, 32):
                    nc.sync.dma_start(
                        out=g2_scales[HALF * par + live : HALF * par + live + 4, groups, par, columns].bitcast(I32),
                        in_=half_scales[HALF * jh + live : HALF * jh + live + 4, groups].bitcast(I32),
                    )

        def keep_g2(groups):
            for par in range(2):
                rows = slice(HALF * par, HALF * (par + 1))
                nc.vector.tensor_copy(
                    out=g2_words[rows, groups, par, rows].bitcast(I32), in_=half_words[rows, groups].bitcast(I32)
                )
                nc.vector.tensor_copy(
                    out=g2_scales[rows, groups, par, rows].bitcast(I32), in_=half_scales[rows, groups].bitcast(I32)
                )

        sums = {}
        d2_tiles = {}
        d2_codes = {}

        def first_core(i, mp):
            words, scales = d1_codes[i]
            sums[mp] = psum.tile([P, CHUNK], F32, tag="bank", name="sums")
            for c in range(2):
                nc.tensor.matmul_mx(
                    out=sums[mp][:],
                    lhsT=g1_words[:, mp // 2, c, mp % 2, :].bitcast(FP8X4),
                    lhsT_scale=g1_scales[:, mp // 2, c, mp % 2, :],
                    rhs=words[:, c, :].bitcast(FP8X4),
                    rhs_scale=scales[:, c, :],
                    start=(c == 0),
                    stop=(c == 1),
                )

        def round_d2(copy, i, mp):
            if mp == 0:
                d2_tiles[i] = d2_pool.tile([P, 2, AG, 4, N_T, PACK], BF16, tag="d2", name="d2", align_bytes=64)
            copy(
                out=d2_tiles[i][:, mp // 4, :, mp % 4],
                in_=sums[mp][:].rearrange("p (ag ai t) -> p ag t ai", ai=PACK, t=N_T),
            )

        def quantise_d2(i):
            words = d2w_pool.tile([P, 2, AG, P], U32, tag="words", name="d2_words", align_bytes=64)
            scales = d2w_pool.tile([P, 2, AG, P], U8, tag="scales", name="d2_scales", align_bytes=64)
            nc.vector.quantize_mx(
                out=words[:].rearrange("p h ag w -> p (h ag w)").bitcast(FP8X4),
                scales=scales[:].rearrange("p h ag w -> p (h ag w)"),
                in_=d2_tiles[i][:].rearrange("p h ag mp t ai -> p (h ag mp t ai)"),
            )
            d2_codes[i] = (words, scales)

        def second_core(i, h):
            words, scales = d2_codes[i]
            for ag in range(AG):
                nc.tensor.matmul_mx(
                    out=terms[h][:],
                    lhsT=words[:, h, ag, :].bitcast(FP8X4),
                    lhsT_scale=scales[:, h, ag, :],
                    rhs=g2_words[:, AG * i + ag].rearrange("p par j -> p (par j)").bitcast(FP8X4),
                    rhs_scale=g2_scales[:, AG * i + ag].rearrange("p par j -> p (par j)"),
                    start=(i == 0 and ag == 0),
                    stop=(i == N_CHUNKS - 1 and ag == AG - 1),
                )

        def out_view(ap):
            return ap.rearrange("b (m0 h q f) -> (b m0) h q f", h=2, q=4, f=256)

        def finish(h):
            result = base[:, h, :]
            nc.vector.tensor_tensor(out=result, in0=result, in1=terms[h][:], op=SUBTRACT)
            for q in range(4):
                queue = nc.sync if q % 2 == 0 else nc.scalar
                queue.dma_start(out=out_view(out)[:, h, q, :], in_=base[N_T * q : N_T * (q + 1), h, :])

        load_d1(0, 1)
        load_g1(0)
        load_g1(1)
        load_d1(1, 1)
        V = nc.vector.tensor_copy
        S = nc.scalar.copy
        nc.vector.memset(warm[:], 0.0)
        S(out=warm[:, 4:8], in_=warm[:, 0:4])
        nc.gpsimd.memset(g2_scales[:].rearrange("p ag par j -> p (ag par j)").bitcast(I32), 0)
        nc.gpsimd.memset(g2_words[0:HALF, 0:16, 1, :], 0)
        nc.vector.memset(half_scales[:].rearrange("p ag j -> p (ag j)").bitcast(I32), 0)
        nc.vector.memset(g2_words[HALF:P, :, 0, :].bitcast(I32), 0)
        nc.vector.memset(g2_words[0:HALF, 16:32, 1, :].bitcast(I32), 0)

        regroup_d1(V, 0, slice(0, 1))
        regroup_d1(V, 0, slice(1, 2))
        regroup_g1(S, 0)
        regroup_g1(V, 1)
        load_d1(2, 1)
        quantise_g1(0)
        load_d1(3, 1)
        quantise_d1(0)
        regroup_g1(S, 2)
        quantise_g1(1)
        load_d1(4, 2)
        load_d1(6, 2)
        load_g2(nc.sync, 0)
        for q in range(4):
            rows = slice(N_T * q, N_T * (q + 1))
            nc.sync.dma_start(out=x_rows[rows], in_=out_view(x_l)[:, :, q, :])
            nc.sync.dma_start(out=mv_rows[rows], in_=out_view(mv)[:, :, q, :])
            for b in range(2):
                nc.sync.dma_start(
                    out=bias_rows[N_T * q + 16 * b : N_T * q + 16 * (b + 1)],
                    in_=bias.rearrange("(m0 h q f) -> m0 h q f", h=2, q=4, f=256)[:, :, q, :],
                )
        regroup_g1(V, 3)
        regroup_d1(V, 1, slice(0, 1))
        quantise_g1(2)
        quantise_g1(3)

        G2_STEPS = {(5, 5): 0, (6, 0): 1, (6, 3): 2, (6, 4): 3}
        for i in range(N_CHUNKS):
            for mp in range(N_MP):
                first_core(i, mp)
                if i == 0 and mp == 1:
                    regroup_d1(S, 1, slice(1, 2))
                round_d2(V if i == 7 and mp == 6 else S, i, mp)
                if mp == (2 if i == 0 else 0) and i + 1 < N_CHUNKS:
                    quantise_d1(i + 1)
                if mp == 1 and i > 0:
                    quantise_d2(i - 1)
                if mp == 2 and i + 2 < N_CHUNKS:
                    regroup_d1(V, i + 2, slice(0, 2))
                if (i, mp - 1) in G2_STEPS:
                    piece = G2_STEPS[(i, mp - 1)]
                    quantise_g2(piece)
                    cross_g2(slice(G2_AG * piece, G2_AG * (piece + 1)))
                if (i, mp) in G2_STEPS:
                    regroup_g2(V if G2_STEPS[(i, mp)] == 3 else S, G2_STEPS[(i, mp)])
                if i == 4 and mp == 0:
                    load_g2(nc.scalar, 1)
                if i == 7 and mp in (2, 5):
                    keep_g2(slice(16 * (mp // 5), 16 * (mp // 5 + 1)))
        quantise_d2(N_CHUNKS - 1)
        nc.vector.tensor_tensor(out=base[:], in0=x_rows[:], in1=mv_rows[:], op=ADD)
        nc.vector.tensor_tensor(out=base[:], in0=base[:], in1=bias_rows[:], op=ADD)
        for i in range(N_CHUNKS):
            for h in range(2):
                second_core(i, h)
        for h in range(2):
            finish(h)
